import numpy as np
import ml_dtypes


def mxq(x, axis, fmt="e4m3"):
    dtype, down = {"e4m3": (ml_dtypes.float8_e4m3fn, 7), "e5m2": (ml_dtypes.float8_e5m2, 14)}[fmt]
    v = np.moveaxis(np.asarray(x, np.float32).astype(ml_dtypes.bfloat16).astype(np.float64), axis, -1)
    blocks = v.reshape(v.shape[:-1] + (-1, 32))
    amax = np.abs(blocks).max(-1, keepdims=True)
    byte = np.maximum(np.where(amax > 0, np.frexp(amax)[1] - 1 + 127, 0) - down, 1)
    scale = np.exp2(byte - 127.0)
    codes = (blocks / scale).astype(np.float32).astype(dtype).astype(np.float64)
    return np.moveaxis((codes * scale).reshape(v.shape), -1, axis)


WIDE = False


def mx_kscale(k):
    if not WIDE:
        return np.ones(k)
    levels = np.array([10, -10, 5, -5, 0])
    a = np.random.permutation(np.resize(levels, k // 512 * 4)).reshape(k // 512, 4)
    idx = np.arange(k)
    return np.exp2(a[idx // 512, idx % 128 // 32])


BF16 = ml_dtypes.bfloat16


def bf(x):
    return np.asarray(x, np.float32).astype(BF16)


def f64(x):
    return np.asarray(x).astype(np.float64)


B, NH, T, D, N = 4, 2, 1024, 128, 1024
THETA = 2.0 ** 16
SCALE = N ** -0.5


def rope_tables():
    pair = np.repeat(np.arange(N // 2), 2)
    freqs = 1.0 / THETA ** (pair * 2.0 / N)
    angles = np.arange(T)[:, None] * freqs[None, :]
    return np.cos(angles), np.sin(angles)


def rope(v, cos, sin):
    v_rot = np.stack([-v[..., 1::2], v[..., ::2]], axis=-1).reshape(v.shape)
    return v * cos + v_rot * sin


def setup_inputs():
    u = mx_kscale(T)
    cos, sin = rope_tables()
    return {"Q": bf(np.random.uniform(size=(B, NH, T, N)) * 1.2 / N ** 0.25 * u[:, None]),
            "V": bf(np.random.standard_normal((B, 1, T, D)) * 45.0 / np.sqrt(T) / u[:, None]),
            "state": bf(np.random.standard_normal((B, NH, N, D)) * 60.0 / N ** 0.75),
            "cos": bf(cos), "sin": bf(sin)}


def reference(Q, V, state, cos, sin):
    QR = rope(f64(Q), f64(cos), f64(sin))
    chunk_state = (np.swapaxes(mxq(QR, 2, "e4m3"), -2, -1) @ mxq(f64(V), 2, "e4m3")) * SCALE
    return f64(state) + chunk_state

@@ -1,0 +1,241 @@
+from contextlib import ExitStack
+
+import concourse.mybir as mybir
+
+F32 = mybir.dt.float32
+BF16 = mybir.dt.bfloat16
+U32 = mybir.dt.uint32
+U8 = mybir.dt.uint8
+FP8X4 = mybir.dt.float8_e4m3fn_x4
+ALU = mybir.AluOpType
+
+B, NH, T, D, N = 4, 2, 1024, 128, 1024
+SCALE = N**-0.5
+FLOPS = 2 * B * NH * T * N * D
+
+P = 128
+PACK = 4
+K_PASS = P * PACK
+PASSES = T // K_PASS
+W_CHUNK = 512
+CHUNKS = N // W_CHUNK
+M_TILES = W_CHUNK // P
+ROUNDS = B * CHUNKS * PASSES
+LOAD_AHEAD = 2
+
+
+def place(r):
+    group, c = divmod(r, PASSES)
+    b, chunk = divmod(group, CHUNKS)
+    return b, chunk, c
+
+
+def tile_attention_pb_t_kernel(tc, Q, V, state, cos, sin, out):
+    nc = tc.nc
+    with ExitStack() as ctx:
+        keep = ctx.enter_context(tc.tile_pool(name="keep", bufs=1))
+        table_pool = ctx.enter_context(tc.tile_pool(name="table_raw", bufs=2))
+        q_pool = ctx.enter_context(tc.tile_pool(name="q_raw", bufs=3))
+        qg_pool = ctx.enter_context(tc.tile_pool(name="q_grouped", bufs=3))
+        m_pool = ctx.enter_context(tc.tile_pool(name="products", bufs=2))
+        g_pool = ctx.enter_context(tc.tile_pool(name="grouped", bufs=3))
+        code_pool = ctx.enter_context(tc.tile_pool(name="codes", bufs=2))
+        batch_pool = ctx.enter_context(tc.tile_pool(name="batch", bufs=2))
+        res_pool = ctx.enter_context(tc.tile_pool(name="res", bufs=4))
+        psum = ctx.enter_context(tc.psum_pool(name="acc", bufs=4))
+
+
+        cos_t = keep.tile([P, PASSES, N, PACK], BF16)
+        sin_t = keep.tile([P, PASSES, N // 2, 2, PACK], BF16)
+
+        q_of = {}
+        tables_of = {}
+        qg_of = {}
+        products_of = {}
+        grouped_of = {}
+        codes_of = {}
+        acc_of = {}
+        v_of = {}
+        state_of = {}
+
+        def load(r):
+            if r >= ROUNDS:
+                return
+            b, chunk, c = place(r)
+            tokens = slice(c * K_PASS, (c + 1) * K_PASS)
+            features = slice(chunk * W_CHUNK, (chunk + 1) * W_CHUNK)
+            q_raw = q_pool.tile([P, NH, PACK, W_CHUNK], BF16)
+            q_of[r] = q_raw
+            for h in range(NH):
+                nc.sync.dma_start(
+                    out=q_raw[:, h],
+                    in_=Q[b, h, tokens, features].rearrange("(p j) w -> p j w", j=PACK),
+                )
+            if b == 0:
+                cos_raw = table_pool.tile([P, PACK, W_CHUNK], BF16)
+                sin_raw = table_pool.tile([P, PACK, W_CHUNK], BF16)
+                tables_of[r] = (cos_raw, sin_raw)
+                for table, table_raw in ((cos, cos_raw), (sin, sin_raw)):
+                    nc.sync.dma_start(
+                        out=table_raw[:],
+                        in_=table[tokens, features].rearrange("(p j) w -> p j w", j=PACK),
+                    )
+            if chunk == 0 and c == 0:
+                v_raw = batch_pool.tile([P, PASSES, PACK, D], BF16)
+                nc.sync.dma_start(
+                    out=v_raw[:], in_=V[b, 0].rearrange("(k p j) d -> p k j d", p=P, j=PACK)
+                )
+                v_grouped = batch_pool.tile([P, PASSES, D, PACK], BF16, align_bytes=64)
+                v_codes = batch_pool.tile([P, PASSES, D], U32, align_bytes=64)
+                v_scales = batch_pool.tile([P, PASSES, D], U8, align_bytes=64)
+                v_of[b] = (v_raw, v_grouped, v_codes, v_scales)
+                state_sb = batch_pool.tile([P, NH, N // P, D], BF16)
+                state_of[b] = state_sb
+                nc.sync.dma_start(
+                    out=state_sb[:], in_=state[b].rearrange("h (m p) d -> p h m d", p=P)
+                )
+
+        def regroup(r):
+            if r >= ROUNDS:
+                return
+            b, chunk, c = place(r)
+            features = slice(chunk * W_CHUNK, (chunk + 1) * W_CHUNK)
+            pairs = slice(chunk * W_CHUNK // 2, (chunk + 1) * W_CHUNK // 2)
+            if r in tables_of:
+                cos_raw, sin_raw = tables_of[r]
+                nc.scalar.copy(
+                    out=cos_t[:, c, features, :], in_=cos_raw[:].rearrange("p j w -> p w j")
+                )
+                by_parity = sin_raw[:].rearrange("p j (i ab) -> p ab i j", ab=2)
+                nc.scalar.mul(out=sin_t[:, c, pairs, 0, :], in_=by_parity[:, 0], mul=-1.0)
+                nc.scalar.copy(out=sin_t[:, c, pairs, 1, :], in_=by_parity[:, 1])
+            q_grouped = qg_pool.tile([P, NH, W_CHUNK // 2, 2, PACK], BF16)
+            qg_of[r] = q_grouped
+            nc.scalar.copy(
+                out=q_grouped[:].rearrange("p h i ab j -> p h (i ab) j"),
+                in_=q_of[r][:].rearrange("p h j w -> p h w j"),
+            )
+            if chunk == 0 and c == 0:
+                v_raw, v_grouped, v_codes, v_scales = v_of[b]
+                nc.scalar.copy(out=v_grouped[:], in_=v_raw[:].rearrange("p k j d -> p k d j"))
+
+        def multiply_tables(r):
+            if r >= ROUNDS:
+                return
+            b, chunk, c = place(r)
+            features = slice(chunk * W_CHUNK, (chunk + 1) * W_CHUNK)
+            pairs = slice(chunk * W_CHUNK // 2, (chunk + 1) * W_CHUNK // 2)
+            q_grouped = qg_of[r]
+            own = m_pool.tile([P, NH, W_CHUNK, PACK], F32)
+            other = m_pool.tile([P, NH, W_CHUNK // 2, 2, PACK], F32)
+            products_of[r] = (own, other)
+            nc.vector.tensor_tensor(
+                out=own[:],
+                in0=q_grouped[:].rearrange("p h i ab j -> p h (i ab) j"),
+                in1=cos_t[:, c, features, :].unsqueeze(1).broadcast_to([P, NH, W_CHUNK, PACK]),
+                op=ALU.mult,
+            )
+            for ab in range(2):
+                nc.vector.tensor_tensor(
+                    out=other[:, :, :, ab, :],
+                    in0=q_grouped[:, :, :, 1 - ab, :],
+                    in1=sin_t[:, c, pairs, ab, :]
+                    .unsqueeze(1)
+                    .broadcast_to([P, NH, W_CHUNK // 2, PACK]),
+                    op=ALU.mult,
+                )
+
+        def add_products(r):
+            if r >= ROUNDS:
+                return
+            own, other = products_of[r]
+            grouped = g_pool.tile([P, NH, W_CHUNK, PACK], BF16, align_bytes=64)
+            grouped_of[r] = grouped
+            nc.vector.tensor_tensor(
+                out=grouped[:],
+                in0=own[:],
+                in1=other[:].rearrange("p h i ab j -> p h (i ab) j"),
+                op=ALU.add,
+            )
+
+        def quantise_v(r):
+            if r >= ROUNDS or r % (CHUNKS * PASSES) != 0:
+                return
+            v_raw, v_grouped, v_codes, v_scales = v_of[place(r)[0]]
+            nc.vector.quantize_mx(
+                out=v_codes[:].rearrange("p k d -> p (k d)").bitcast(FP8X4),
+                scales=v_scales[:].rearrange("p k d -> p (k d)"),
+                in_=v_grouped[:].rearrange("p k d j -> p (k d j)"),
+            )
+
+        def quantise(r):
+            if r < 0 or r >= ROUNDS:
+                return
+            b, chunk, c = place(r)
+            if c == 0:
+                qr_codes = code_pool.tile([P, PASSES, NH, W_CHUNK], U32, align_bytes=64)
+                qr_scales = code_pool.tile([P, PASSES, NH, W_CHUNK], U8, align_bytes=64)
+                codes_of[(b, chunk)] = (qr_codes, qr_scales)
+            qr_codes, qr_scales = codes_of[(b, chunk)]
+            for h in range(NH):
+                nc.vector.quantize_mx(
+                    out=qr_codes[:, c, h, :].bitcast(FP8X4),
+                    scales=qr_scales[:, c, h, :],
+                    in_=grouped_of[r][:, h].rearrange("p w j -> p (w j)"),
+                )
+
+        def multiply(r):
+            if r < 0 or r >= ROUNDS or place(r)[2] != PASSES - 1:
+                return
+            b, chunk, c = place(r)
+            qr_codes, qr_scales = codes_of[(b, chunk)]
+            v_raw, v_grouped, v_codes, v_scales = v_of[b]
+            acc_of[(b, chunk)] = []
+            for h in range(NH):
+                acc = psum.tile([P, M_TILES, D], F32)
+                acc_of[(b, chunk)].append(acc)
+                for m in range(M_TILES):
+                    columns = slice(m * P, (m + 1) * P)
+                    for k in range(PASSES):
+                        nc.tensor.matmul_mx(
+                            out=acc[:, m, :],
+                            lhsT=qr_codes[:, k, h, columns].bitcast(FP8X4),
+                            lhsT_scale=qr_scales[:, k, h, columns],
+                            rhs=v_codes[:, k, :].bitcast(FP8X4),
+                            rhs_scale=v_scales[:, k, :],
+                            start=(k == 0),
+                            stop=(k == PASSES - 1),
+                        )
+
+        def add_state(r):
+            if r < 0 or r >= ROUNDS or place(r)[2] != PASSES - 1:
+                return
+            b, chunk, c = place(r)
+            features = slice(chunk * W_CHUNK, (chunk + 1) * W_CHUNK)
+            for h in range(NH):
+                res = res_pool.tile([P, M_TILES, D], F32)
+                nc.vector.scalar_tensor_tensor(
+                    out=res[:],
+                    in0=acc_of[(b, chunk)][h][:],
+                    scalar=SCALE,
+                    in1=state_of[b][:, h, chunk * M_TILES : (chunk + 1) * M_TILES, :],
+                    op0=ALU.mult,
+                    op1=ALU.add,
+                )
+                nc.sync.dma_start(
+                    out=out[b, h, features, :].rearrange("(m p) d -> p m d", p=P), in_=res[:]
+                )
+
+        with tc.manual_schedule():
+            for r in range(LOAD_AHEAD):
+                load(r)
+            regroup(0)
+            for step in range(ROUNDS + 2):
+                load(step + LOAD_AHEAD)
+                regroup(step + 1)
+                multiply_tables(step)
+                add_state(step - 2)
+                quantise(step - 1)
+                multiply(step - 1)
+                add_products(step)
+                quantise_v(step)

@@ -1,6 +1,7 @@
 from contextlib import ExitStack
 
 import concourse.mybir as mybir
+from concourse.masks import make_identity
 
 F32 = mybir.dt.float32
 BF16 = mybir.dt.bfloat16
@@ -17,225 +18,295 @@ P = 128
 PACK = 4
 K_PASS = P * PACK
 PASSES = T // K_PASS
-W_CHUNK = 512
-CHUNKS = N // W_CHUNK
-M_TILES = W_CHUNK // P
-ROUNDS = B * CHUNKS * PASSES
-LOAD_AHEAD = 2
+W_UNIT = 2 * P
+UNITS = 2
+W_ROUND = UNITS * W_UNIT
+GROUPS = N // W_ROUND
+HEADS = B * NH
+BLOCK_ROUNDS = HEADS
+ROUNDS = GROUPS * PASSES * BLOCK_ROUNDS
+BLOCKS = GROUPS * PASSES
+ALL_UNITS = ROUNDS * UNITS
+BLOCK_UNITS = BLOCK_ROUNDS * UNITS
+LOAD_AHEAD = 3
+X = K_PASS
+XV = 320
 
 
 def place(r):
-    group, c = divmod(r, PASSES)
-    b, chunk = divmod(group, CHUNKS)
-    return b, chunk, c
+    blk, bh = divmod(r, BLOCK_ROUNDS)
+    g, c = divmod(blk, PASSES)
+    b, h = divmod(bh, NH)
+    return blk, g, c, b, h
 
 
 def tile_attention_pb_t_kernel(tc, Q, V, state, cos, sin, out):
     nc = tc.nc
     with ExitStack() as ctx:
         keep = ctx.enter_context(tc.tile_pool(name="keep", bufs=1))
-        table_pool = ctx.enter_context(tc.tile_pool(name="table_raw", bufs=2))
-        q_pool = ctx.enter_context(tc.tile_pool(name="q_raw", bufs=3))
-        qg_pool = ctx.enter_context(tc.tile_pool(name="q_grouped", bufs=3))
-        m_pool = ctx.enter_context(tc.tile_pool(name="products", bufs=2))
-        g_pool = ctx.enter_context(tc.tile_pool(name="grouped", bufs=3))
-        code_pool = ctx.enter_context(tc.tile_pool(name="codes", bufs=2))
-        batch_pool = ctx.enter_context(tc.tile_pool(name="batch", bufs=2))
+        raw_pool = ctx.enter_context(tc.tile_pool(name="table_raw", bufs=2))
+        table_pool = ctx.enter_context(tc.tile_pool(name="tables", bufs=BLOCKS * UNITS))
+        q_pool = ctx.enter_context(tc.tile_pool(name="q_raw", bufs=5))
+        qs_pool = ctx.enter_context(tc.tile_pool(name="q_share", bufs=3))
+        prod_pool = ctx.enter_context(tc.tile_pool(name="products", bufs=3))
+        g_pool = ctx.enter_context(tc.tile_pool(name="grouped", bufs=4))
+        first_pool = ctx.enter_context(tc.tile_pool(name="codes_first", bufs=HEADS + 2))
+        last_pool = ctx.enter_context(tc.tile_pool(name="codes_last", bufs=3))
+        v_pool = ctx.enter_context(tc.tile_pool(name="v", bufs=B))
+        state_pool = ctx.enter_context(tc.tile_pool(name="state", bufs=6))
         res_pool = ctx.enter_context(tc.tile_pool(name="res", bufs=4))
-        psum = ctx.enter_context(tc.psum_pool(name="acc", bufs=4))
+        qt_psum = ctx.enter_context(tc.psum_pool(name="qt_psum", bufs=3))
+        sum_psum = ctx.enter_context(tc.psum_pool(name="sum_psum", bufs=4))
+        acc_psum = ctx.enter_context(tc.psum_pool(name="acc_psum", bufs=1))
 
+        ident = keep.tile([P, P], F32)
+        make_identity(nc, ident[:])
 
-        cos_t = keep.tile([P, PASSES, N, PACK], BF16)
-        sin_t = keep.tile([P, PASSES, N // 2, 2, PACK], BF16)
+        q_of, raw_of, table_of, qt_of, qs_of, prod_of = {}, {}, {}, {}, {}, {}
+        sum_of, grouped_of, codes_of, acc_of, v_of, state_of = {}, {}, {}, {}, {}, {}
 
-        q_of = {}
-        tables_of = {}
-        qg_of = {}
-        products_of = {}
-        grouped_of = {}
-        codes_of = {}
-        acc_of = {}
-        v_of = {}
-        state_of = {}
-
-        def load(r):
-            if r >= ROUNDS:
-                return
-            b, chunk, c = place(r)
+        def load_tables(blk, k):
+            g, c = divmod(blk, PASSES)
             tokens = slice(c * K_PASS, (c + 1) * K_PASS)
-            features = slice(chunk * W_CHUNK, (chunk + 1) * W_CHUNK)
-            q_raw = q_pool.tile([P, NH, PACK, W_CHUNK], BF16)
+            w0 = g * W_ROUND + k * W_UNIT
+            cos_raw = raw_pool.tile([P, PACK, W_UNIT], BF16)
+            sin_raw = raw_pool.tile([P, PACK, W_UNIT], BF16)
+            raw_of[(blk, k)] = (cos_raw, sin_raw)
+            for table, table_raw in ((cos, cos_raw), (sin, sin_raw)):
+                nc.sync.dma_start(
+                    out=table_raw[:],
+                    in_=table[tokens, w0 : w0 + W_UNIT].rearrange("(p j) w -> p j w", j=PACK),
+                )
+
+        def load_q(r, split):
+            if r >= ROUNDS:
+                return
+            blk, g, c, b, h = place(r)
+            tokens = slice(c * K_PASS, (c + 1) * K_PASS)
+            q_raw = q_pool.tile([P, PACK, W_ROUND], BF16)
             q_of[r] = q_raw
-            for h in range(NH):
+            width = W_ROUND // split
+            for i in range(split):
+                w0 = g * W_ROUND + i * width
                 nc.sync.dma_start(
-                    out=q_raw[:, h],
-                    in_=Q[b, h, tokens, features].rearrange("(p j) w -> p j w", j=PACK),
+                    out=q_raw[:, :, i * width : (i + 1) * width],
+                    in_=Q[b, h, tokens, w0 : w0 + width].rearrange("(p j) w -> p j w", j=PACK),
                 )
-            if b == 0:
-                cos_raw = table_pool.tile([P, PACK, W_CHUNK], BF16)
-                sin_raw = table_pool.tile([P, PACK, W_CHUNK], BF16)
-                tables_of[r] = (cos_raw, sin_raw)
-                for table, table_raw in ((cos, cos_raw), (sin, sin_raw)):
-                    nc.sync.dma_start(
-                        out=table_raw[:],
-                        in_=table[tokens, features].rearrange("(p j) w -> p j w", j=PACK),
-                    )
-            if chunk == 0 and c == 0:
-                v_raw = batch_pool.tile([P, PASSES, PACK, D], BF16)
+            if c == PASSES - 1:
+                state_sb = state_pool.tile([P, UNITS, 2, D], BF16)
+                state_of[r] = state_sb
                 nc.sync.dma_start(
-                    out=v_raw[:], in_=V[b, 0].rearrange("(k p j) d -> p k j d", p=P, j=PACK)
-                )
-                v_grouped = batch_pool.tile([P, PASSES, D, PACK], BF16, align_bytes=64)
-                v_codes = batch_pool.tile([P, PASSES, D], U32, align_bytes=64)
-                v_scales = batch_pool.tile([P, PASSES, D], U8, align_bytes=64)
-                v_of[b] = (v_raw, v_grouped, v_codes, v_scales)
-                state_sb = batch_pool.tile([P, NH, N // P, D], BF16)
-                state_of[b] = state_sb
-                nc.sync.dma_start(
-                    out=state_sb[:], in_=state[b].rearrange("h (m p) d -> p h m d", p=P)
+                    out=state_sb[:],
+                    in_=state[b, h, g * W_ROUND : (g + 1) * W_ROUND, :].rearrange(
+                        "(k i ab) d -> i k ab d", k=UNITS, ab=2
+                    ),
                 )
 
-        def regroup(r):
-            if r >= ROUNDS:
-                return
-            b, chunk, c = place(r)
-            features = slice(chunk * W_CHUNK, (chunk + 1) * W_CHUNK)
-            pairs = slice(chunk * W_CHUNK // 2, (chunk + 1) * W_CHUNK // 2)
-            if r in tables_of:
-                cos_raw, sin_raw = tables_of[r]
-                nc.scalar.copy(
-                    out=cos_t[:, c, features, :], in_=cos_raw[:].rearrange("p j w -> p w j")
-                )
-                by_parity = sin_raw[:].rearrange("p j (i ab) -> p ab i j", ab=2)
-                nc.scalar.mul(out=sin_t[:, c, pairs, 0, :], in_=by_parity[:, 0], mul=-1.0)
-                nc.scalar.copy(out=sin_t[:, c, pairs, 1, :], in_=by_parity[:, 1])
-            q_grouped = qg_pool.tile([P, NH, W_CHUNK // 2, 2, PACK], BF16)
-            qg_of[r] = q_grouped
-            nc.scalar.copy(
-                out=q_grouped[:].rearrange("p h i ab j -> p h (i ab) j"),
-                in_=q_of[r][:].rearrange("p h j w -> p h w j"),
+        def load_v(b):
+            v_raw = v_pool.tile([P, PASSES, PACK, D], BF16)
+            nc.sync.dma_start(
+                out=v_raw[:], in_=V[b, 0].rearrange("(c p j) d -> p c j d", p=P, j=PACK)
             )
-            if chunk == 0 and c == 0:
-                v_raw, v_grouped, v_codes, v_scales = v_of[b]
-                nc.scalar.copy(out=v_grouped[:], in_=v_raw[:].rearrange("p k j d -> p k d j"))
+            v_of[b] = [v_raw]
 
-        def multiply_tables(r):
-            if r >= ROUNDS:
-                return
-            b, chunk, c = place(r)
-            features = slice(chunk * W_CHUNK, (chunk + 1) * W_CHUNK)
-            pairs = slice(chunk * W_CHUNK // 2, (chunk + 1) * W_CHUNK // 2)
-            q_grouped = qg_of[r]
-            own = m_pool.tile([P, NH, W_CHUNK, PACK], F32)
-            other = m_pool.tile([P, NH, W_CHUNK // 2, 2, PACK], F32)
-            products_of[r] = (own, other)
-            nc.vector.tensor_tensor(
-                out=own[:],
-                in0=q_grouped[:].rearrange("p h i ab j -> p h (i ab) j"),
-                in1=cos_t[:, c, features, :].unsqueeze(1).broadcast_to([P, NH, W_CHUNK, PACK]),
-                op=ALU.mult,
+        def group_v(b):
+            v_grouped = v_pool.tile([P, PASSES, D, PACK], BF16, align_bytes=64)
+            nc.scalar.copy(out=v_grouped[:], in_=v_of[b][0][:].rearrange("p c j d -> p c d j"))
+            v_of[b].append(v_grouped)
+
+        def quantise_v(b):
+            v_codes = v_pool.tile([P, PASSES, D], U32, align_bytes=64)
+            v_scales = v_pool.tile([P, PASSES, D], U8, align_bytes=64)
+            nc.vector.quantize_mx(
+                out=v_codes[:].rearrange("p c d -> p (c d)").bitcast(FP8X4),
+                scales=v_scales[:].rearrange("p c d -> p (c d)"),
+                in_=v_of[b][1][:].rearrange("p c d j -> p (c d j)"),
             )
-            for ab in range(2):
-                nc.vector.tensor_tensor(
-                    out=other[:, :, :, ab, :],
-                    in0=q_grouped[:, :, :, 1 - ab, :],
-                    in1=sin_t[:, c, pairs, ab, :]
+            v_of[b] = (v_codes, v_scales)
+
+        def turn_table(blk, k, which):
+            if (blk, k) not in table_of:
+                table = table_pool.tile([P, 2, 2, X], BF16)
+                table_of[(blk, k)] = table
+            table_t = table_of[(blk, k)]
+            table_raw = raw_of[(blk, k)][which]
+            qt = qt_psum.tile([P, X], F32)
+            for j in range(PACK):
+                nc.tensor.transpose(
+                    qt[:, j * P : (j + 1) * P], table_raw[:, j, :].bitcast(F32), ident[:]
+                )
+            by_parity = qt[:].bitcast(BF16).rearrange("i (x ab) -> i ab x", ab=2)
+            if which == 0:
+                if blk == 0:
+                    nc.vector.tensor_copy(out=table_t[:, 0], in_=by_parity)
+                else:
+                    nc.scalar.copy(out=table_t[:, 0], in_=by_parity)
+            else:
+                nc.scalar.copy(out=table_t[:, 1, 0, :], in_=by_parity[:, 1])
+                nc.scalar.mul(out=table_t[:, 1, 1, :], in_=by_parity[:, 0], mul=-1.0)
+
+        def turn_q(u):
+            if u >= ALL_UNITS:
+                return
+            r, k = divmod(u, UNITS)
+            qt = qt_psum.tile([P, X], F32)
+            qt_of[u] = qt
+            for j in range(PACK):
+                nc.tensor.transpose(
+                    qt[:, j * P : (j + 1) * P],
+                    q_of[r][:, j, k * W_UNIT : (k + 1) * W_UNIT].bitcast(F32),
+                    ident[:],
+                )
+
+        def share_q(u):
+            if u >= ALL_UNITS:
+                return
+            q_share = qs_pool.tile([P, X - XV], F32)
+            qs_of[u] = q_share
+            nc.scalar.copy(out=q_share[:], in_=qt_of[u][:, XV:])
+
+        def products(u):
+            if u >= ALL_UNITS:
+                return
+            r, k = divmod(u, UNITS)
+            table_t = table_of[(place(r)[0], k)]
+            prod = prod_pool.tile([P, 2, 2, X], F32)
+            prod_of[u] = prod
+            for engine, q_words, x0, x1 in (
+                (nc.vector, qt_of[u][:, :XV], 0, XV),
+                (nc.gpsimd, qs_of[u][:], XV, X),
+            ):
+                engine.tensor_tensor(
+                    out=prod[:, :, :, x0:x1],
+                    in0=q_words.bitcast(BF16)
+                    .rearrange("i (x ab) -> i ab x", ab=2)
                     .unsqueeze(1)
-                    .broadcast_to([P, NH, W_CHUNK // 2, PACK]),
+                    .broadcast_to([P, 2, 2, x1 - x0]),
+                    in1=table_t[:, :, :, x0:x1],
                     op=ALU.mult,
                 )
 
-        def add_products(r):
-            if r >= ROUNDS:
+        def sums(u):
+            if u < 0 or u >= ALL_UNITS:
                 return
-            own, other = products_of[r]
-            grouped = g_pool.tile([P, NH, W_CHUNK, PACK], BF16, align_bytes=64)
-            grouped_of[r] = grouped
-            nc.vector.tensor_tensor(
-                out=grouped[:],
-                in0=own[:],
-                in1=other[:].rearrange("p h i ab j -> p h (i ab) j"),
-                op=ALU.add,
-            )
+            prod = prod_of[u]
+            sum_of[u] = []
+            for ab in range(2):
+                acc_sum = sum_psum.tile([P, PACK, P], F32)
+                sum_of[u].append(acc_sum)
+                for j in range(PACK):
+                    tokens = slice(j * P, (j + 1) * P)
+                    nc.tensor.matmul(
+                        acc_sum[:, j, :], prod[:, 0, ab, tokens], ident[:],
+                        start=True, stop=False, is_transpose=True,
+                    )
+                    nc.tensor.matmul(
+                        acc_sum[:, j, :], prod[:, 1, 1 - ab, tokens], ident[:],
+                        start=False, stop=True, is_transpose=True,
+                    )
 
-        def quantise_v(r):
-            if r >= ROUNDS or r % (CHUNKS * PASSES) != 0:
+        def regroup(u):
+            if u < 0 or u >= ALL_UNITS:
                 return
-            v_raw, v_grouped, v_codes, v_scales = v_of[place(r)[0]]
-            nc.vector.quantize_mx(
-                out=v_codes[:].rearrange("p k d -> p (k d)").bitcast(FP8X4),
-                scales=v_scales[:].rearrange("p k d -> p (k d)"),
-                in_=v_grouped[:].rearrange("p k d j -> p (k d j)"),
-            )
-
-        def quantise(r):
-            if r < 0 or r >= ROUNDS:
-                return
-            b, chunk, c = place(r)
-            if c == 0:
-                qr_codes = code_pool.tile([P, PASSES, NH, W_CHUNK], U32, align_bytes=64)
-                qr_scales = code_pool.tile([P, PASSES, NH, W_CHUNK], U8, align_bytes=64)
-                codes_of[(b, chunk)] = (qr_codes, qr_scales)
-            qr_codes, qr_scales = codes_of[(b, chunk)]
-            for h in range(NH):
-                nc.vector.quantize_mx(
-                    out=qr_codes[:, c, h, :].bitcast(FP8X4),
-                    scales=qr_scales[:, c, h, :],
-                    in_=grouped_of[r][:, h].rearrange("p w j -> p (w j)"),
+            grouped = g_pool.tile([P, 2, P, PACK], BF16, align_bytes=64)
+            grouped_of[u] = grouped
+            for ab in range(2):
+                nc.scalar.copy(
+                    out=grouped[:, ab], in_=sum_of[u][ab][:].rearrange("p j i -> p i j")
                 )
+
+        def quantise(u):
+            if u < 0 or u >= ALL_UNITS:
+                return
+            r, k = divmod(u, UNITS)
+            blk, g, c, b, h = place(r)
+            key = (g, c, b, h)
+            if k == 0:
+                pool = first_pool if c == 0 else last_pool
+                codes = pool.tile([P, UNITS, 2, P], U32, align_bytes=64)
+                scales = pool.tile([P, UNITS, 2, P], U8, align_bytes=64)
+                codes_of[key] = (codes, scales)
+            codes, scales = codes_of[key]
+            nc.vector.quantize_mx(
+                out=codes[:, k].rearrange("p ab i -> p (ab i)").bitcast(FP8X4),
+                scales=scales[:, k].rearrange("p ab i -> p (ab i)"),
+                in_=grouped_of[u][:].rearrange("p ab i j -> p (ab i j)"),
+            )
 
         def multiply(r):
             if r < 0 or r >= ROUNDS or place(r)[2] != PASSES - 1:
                 return
-            b, chunk, c = place(r)
-            qr_codes, qr_scales = codes_of[(b, chunk)]
-            v_raw, v_grouped, v_codes, v_scales = v_of[b]
-            acc_of[(b, chunk)] = []
-            for h in range(NH):
-                acc = psum.tile([P, M_TILES, D], F32)
-                acc_of[(b, chunk)].append(acc)
-                for m in range(M_TILES):
-                    columns = slice(m * P, (m + 1) * P)
-                    for k in range(PASSES):
+            blk, g, c, b, h = place(r)
+            v_codes, v_scales = v_of[b]
+            acc = acc_psum.tile([P, UNITS, 2, D], F32)
+            acc_of[r] = acc
+            for k in range(UNITS):
+                for ab in range(2):
+                    for t in range(PASSES):
+                        codes, scales = codes_of[(g, t, b, h)]
                         nc.tensor.matmul_mx(
-                            out=acc[:, m, :],
-                            lhsT=qr_codes[:, k, h, columns].bitcast(FP8X4),
-                            lhsT_scale=qr_scales[:, k, h, columns],
-                            rhs=v_codes[:, k, :].bitcast(FP8X4),
-                            rhs_scale=v_scales[:, k, :],
-                            start=(k == 0),
-                            stop=(k == PASSES - 1),
+                            out=acc[:, k, ab, :],
+                            lhsT=codes[:, k, ab, :].bitcast(FP8X4),
+                            lhsT_scale=scales[:, k, ab, :],
+                            rhs=v_codes[:, t, :].bitcast(FP8X4),
+                            rhs_scale=v_scales[:, t, :],
+                            start=(t == 0),
+                            stop=(t == PASSES - 1),
                         )
 
         def add_state(r):
             if r < 0 or r >= ROUNDS or place(r)[2] != PASSES - 1:
                 return
-            b, chunk, c = place(r)
-            features = slice(chunk * W_CHUNK, (chunk + 1) * W_CHUNK)
-            for h in range(NH):
-                res = res_pool.tile([P, M_TILES, D], F32)
-                nc.vector.scalar_tensor_tensor(
-                    out=res[:],
-                    in0=acc_of[(b, chunk)][h][:],
-                    scalar=SCALE,
-                    in1=state_of[b][:, h, chunk * M_TILES : (chunk + 1) * M_TILES, :],
-                    op0=ALU.mult,
-                    op1=ALU.add,
-                )
-                nc.sync.dma_start(
-                    out=out[b, h, features, :].rearrange("(m p) d -> p m d", p=P), in_=res[:]
-                )
+            blk, g, c, b, h = place(r)
+            res = res_pool.tile([P, UNITS, 2, D], F32)
+            nc.vector.scalar_tensor_tensor(
+                out=res[:],
+                in0=acc_of[r][:],
+                scalar=SCALE,
+                in1=state_of[r][:],
+                op0=ALU.mult,
+                op1=ALU.add,
+            )
+            nc.sync.dma_start(
+                out=out[b, h, g * W_ROUND : (g + 1) * W_ROUND, :].rearrange(
+                    "(k i ab) d -> i k ab d", k=UNITS, ab=2
+                ),
+                in_=res[:],
+            )
 
         with tc.manual_schedule():
-            for r in range(LOAD_AHEAD):
-                load(r)
-            regroup(0)
-            for step in range(ROUNDS + 2):
-                load(step + LOAD_AHEAD)
-                regroup(step + 1)
-                multiply_tables(step)
-                add_state(step - 2)
-                quantise(step - 1)
-                multiply(step - 1)
-                add_products(step)
-                quantise_v(step)
+            load_tables(0, 0)
+            load_q(0, UNITS)
+            load_tables(0, 1)
+            for r in range(1, LOAD_AHEAD):
+                load_q(r, 1)
+            turn_table(0, 0, 0)
+            turn_table(0, 0, 1)
+            turn_q(0)
+            share_q(0)
+            turn_table(0, 1, 0)
+            turn_table(0, 1, 1)
+            turn_q(1)
+            for s in range(ALL_UNITS + 6):
+                blk, in_block = divmod(s, BLOCK_UNITS)
+                if s % UNITS == 0:
+                    load_q(s // UNITS + LOAD_AHEAD, 1)
+                if blk == 0 and in_block in (3, 5, 7, 9):
+                    load_v((in_block - 3) // 2)
+                if blk + 1 < BLOCKS and in_block in (2, 4):
+                    load_tables(blk + 1, (in_block - 2) // 2)
+                sums(s - 1)
+                if blk + 1 < BLOCKS and in_block in (7, 9, 11, 13):
+                    turn_table(blk + 1, (in_block - 7) // 4, (in_block - 7) // 2 % 2)
+                turn_q(s + 2)
+                share_q(s + 1)
+                products(s)
+                regroup(s - 1)
+                if blk == 0 and in_block in (6, 8, 10, 12):
+                    group_v((in_block - 6) // 2)
+                quantise(s - 2)
+                if blk == 0 and in_block in (7, 9, 11, 13):
+                    quantise_v((in_block - 7) // 2)
+                if s % UNITS == 0:
+                    multiply(s // UNITS - 2)
+                    add_state(s // UNITS - 2)

@@ -23,34 +23,34 @@ UNITS = 2
 W_ROUND = UNITS * W_UNIT
 GROUPS = N // W_ROUND
 HEADS = B * NH
-BLOCK_ROUNDS = HEADS
-ROUNDS = GROUPS * PASSES * BLOCK_ROUNDS
-BLOCKS = GROUPS * PASSES
+ROUNDS = GROUPS * HEADS * PASSES
 ALL_UNITS = ROUNDS * UNITS
-BLOCK_UNITS = BLOCK_ROUNDS * UNITS
+GROUP_UNITS = HEADS * PASSES * UNITS
+TABLES = PASSES * UNITS
 LOAD_AHEAD = 3
+KEEP_UP = 92
 X = K_PASS
 XV = 320
 
 
 def place(r):
-    blk, bh = divmod(r, BLOCK_ROUNDS)
-    g, c = divmod(blk, PASSES)
+    rest, c = divmod(r, PASSES)
+    g, bh = divmod(rest, HEADS)
     b, h = divmod(bh, NH)
-    return blk, g, c, b, h
+    return g, c, b, h
 
 
 def tile_attention_pb_t_kernel(tc, Q, V, state, cos, sin, out):
     nc = tc.nc
     with ExitStack() as ctx:
         keep = ctx.enter_context(tc.tile_pool(name="keep", bufs=1))
-        raw_pool = ctx.enter_context(tc.tile_pool(name="table_raw", bufs=2))
-        table_pool = ctx.enter_context(tc.tile_pool(name="tables", bufs=BLOCKS * UNITS))
+        raw_pool = ctx.enter_context(tc.tile_pool(name="table_raw", bufs=TABLES))
+        table_pool = ctx.enter_context(tc.tile_pool(name="tables", bufs=GROUPS * TABLES))
         q_pool = ctx.enter_context(tc.tile_pool(name="q_raw", bufs=5))
         qs_pool = ctx.enter_context(tc.tile_pool(name="q_share", bufs=3))
         prod_pool = ctx.enter_context(tc.tile_pool(name="products", bufs=3))
         g_pool = ctx.enter_context(tc.tile_pool(name="grouped", bufs=4))
-        first_pool = ctx.enter_context(tc.tile_pool(name="codes_first", bufs=HEADS + 2))
+        first_pool = ctx.enter_context(tc.tile_pool(name="codes_first", bufs=3))
         last_pool = ctx.enter_context(tc.tile_pool(name="codes_last", bufs=3))
         v_pool = ctx.enter_context(tc.tile_pool(name="v", bufs=B))
         state_pool = ctx.enter_context(tc.tile_pool(name="state", bufs=6))
@@ -65,13 +65,13 @@ def tile_attention_pb_t_kernel(tc, Q, V, state, cos, sin, out):
         q_of, raw_of, table_of, qt_of, qs_of, prod_of = {}, {}, {}, {}, {}, {}
         sum_of, grouped_of, codes_of, acc_of, v_of, state_of = {}, {}, {}, {}, {}, {}
 
-        def load_tables(blk, k):
-            g, c = divmod(blk, PASSES)
+        def load_tables(g, i):
+            c, k = divmod(i, UNITS)
             tokens = slice(c * K_PASS, (c + 1) * K_PASS)
             w0 = g * W_ROUND + k * W_UNIT
             cos_raw = raw_pool.tile([P, PACK, W_UNIT], BF16)
             sin_raw = raw_pool.tile([P, PACK, W_UNIT], BF16)
-            raw_of[(blk, k)] = (cos_raw, sin_raw)
+            raw_of[(g, c, k)] = (cos_raw, sin_raw)
             for table, table_raw in ((cos, cos_raw), (sin, sin_raw)):
                 nc.sync.dma_start(
                     out=table_raw[:],
@@ -81,7 +81,7 @@ def tile_attention_pb_t_kernel(tc, Q, V, state, cos, sin, out):
         def load_q(r, split):
             if r >= ROUNDS:
                 return
-            blk, g, c, b, h = place(r)
+            g, c, b, h = place(r)
             tokens = slice(c * K_PASS, (c + 1) * K_PASS)
             q_raw = q_pool.tile([P, PACK, W_ROUND], BF16)
             q_of[r] = q_raw
@@ -124,20 +124,22 @@ def tile_attention_pb_t_kernel(tc, Q, V, state, cos, sin, out):
             )
             v_of[b] = (v_codes, v_scales)
 
-        def turn_table(blk, k, which):
-            if (blk, k) not in table_of:
-                table = table_pool.tile([P, 2, 2, X], BF16)
-                table_of[(blk, k)] = table
-            table_t = table_of[(blk, k)]
-            table_raw = raw_of[(blk, k)][which]
-            qt = qt_psum.tile([P, X], F32)
-            for j in range(PACK):
-                nc.tensor.transpose(
-                    qt[:, j * P : (j + 1) * P], table_raw[:, j, :].bitcast(F32), ident[:]
-                )
-            by_parity = qt[:].bitcast(BF16).rearrange("i (x ab) -> i ab x", ab=2)
+        def turn_table(g, i, which):
+            key = (g, *divmod(i, UNITS))
             if which == 0:
-                if blk == 0:
+                table_t = table_pool.tile([P, 2, 2, X], BF16)
+                table_of[key] = table_t
+            table_t = table_of[key]
+            table_raw = raw_of[key][which]
+            bank = sum_psum.tile([P, PACK, P], F32, tag="sum")
+            for j in range(PACK):
+                nc.tensor.transpose(bank[:, j, :], table_raw[:, j, :].bitcast(F32), ident[:])
+            by_parity = (
+                bank[:].rearrange("i j p -> i (j p)").bitcast(BF16)
+                .rearrange("i (x ab) -> i ab x", ab=2)
+            )
+            if which == 0:
+                if g == 0:
                     nc.vector.tensor_copy(out=table_t[:, 0], in_=by_parity)
                 else:
                     nc.scalar.copy(out=table_t[:, 0], in_=by_parity)
@@ -169,7 +171,8 @@ def tile_attention_pb_t_kernel(tc, Q, V, state, cos, sin, out):
             if u >= ALL_UNITS:
                 return
             r, k = divmod(u, UNITS)
-            table_t = table_of[(place(r)[0], k)]
+            g, c, b, h = place(r)
+            table_t = table_of[(g, c, k)]
             prod = prod_pool.tile([P, 2, 2, X], F32)
             prod_of[u] = prod
             for engine, q_words, x0, x1 in (
@@ -192,8 +195,12 @@ def tile_attention_pb_t_kernel(tc, Q, V, state, cos, sin, out):
             prod = prod_of[u]
             sum_of[u] = []
             for ab in range(2):
-                acc_sum = sum_psum.tile([P, PACK, P], F32)
+                acc_sum = sum_psum.tile([P, PACK, P], F32, tag="sum")
                 sum_of[u].append(acc_sum)
+                if ab == 0:
+                    nc.tensor.matmul(
+                        acc_sum[:, 0, :KEEP_UP], ident[:], ident[:, :KEEP_UP], start=True, stop=True
+                    )
                 for j in range(PACK):
                     tokens = slice(j * P, (j + 1) * P)
                     nc.tensor.matmul(
@@ -219,7 +226,7 @@ def tile_attention_pb_t_kernel(tc, Q, V, state, cos, sin, out):
             if u < 0 or u >= ALL_UNITS:
                 return
             r, k = divmod(u, UNITS)
-            blk, g, c, b, h = place(r)
+            g, c, b, h = place(r)
             key = (g, c, b, h)
             if k == 0:
                 pool = first_pool if c == 0 else last_pool
@@ -234,9 +241,9 @@ def tile_attention_pb_t_kernel(tc, Q, V, state, cos, sin, out):
             )
 
         def multiply(r):
-            if r < 0 or r >= ROUNDS or place(r)[2] != PASSES - 1:
+            if r < 0 or r >= ROUNDS or place(r)[1] != PASSES - 1:
                 return
-            blk, g, c, b, h = place(r)
+            g, c, b, h = place(r)
             v_codes, v_scales = v_of[b]
             acc = acc_psum.tile([P, UNITS, 2, D], F32)
             acc_of[r] = acc
@@ -255,9 +262,9 @@ def tile_attention_pb_t_kernel(tc, Q, V, state, cos, sin, out):
                         )
 
         def add_state(r):
-            if r < 0 or r >= ROUNDS or place(r)[2] != PASSES - 1:
+            if r < 0 or r >= ROUNDS or place(r)[1] != PASSES - 1:
                 return
-            blk, g, c, b, h = place(r)
+            g, c, b, h = place(r)
             res = res_pool.tile([P, UNITS, 2, D], F32)
             nc.vector.scalar_tensor_tensor(
                 out=res[:],
@@ -275,11 +282,21 @@ def tile_attention_pb_t_kernel(tc, Q, V, state, cos, sin, out):
             )
 
         with tc.manual_schedule():
+            warm = sum_psum.tile([P, PACK, P], F32, tag="sum")
+            nc.tensor.matmul(
+                warm[:],
+                ident[:],
+                ident[:].unsqueeze(1).broadcast_to([P, PACK, P]),
+                start=True, stop=True,
+            )
             load_tables(0, 0)
             load_q(0, UNITS)
             load_tables(0, 1)
-            for r in range(1, LOAD_AHEAD):
-                load_q(r, 1)
+            load_q(1, 1)
+            load_v(0)
+            load_tables(0, 2)
+            load_tables(0, 3)
+            load_q(2, 1)
             turn_table(0, 0, 0)
             turn_table(0, 0, 1)
             turn_q(0)
@@ -288,25 +305,27 @@ def tile_attention_pb_t_kernel(tc, Q, V, state, cos, sin, out):
             turn_table(0, 1, 1)
             turn_q(1)
             for s in range(ALL_UNITS + 6):
-                blk, in_block = divmod(s, BLOCK_UNITS)
                 if s % UNITS == 0:
                     load_q(s // UNITS + LOAD_AHEAD, 1)
-                if blk == 0 and in_block in (3, 5, 7, 9):
-                    load_v((in_block - 3) // 2)
-                if blk + 1 < BLOCKS and in_block in (2, 4):
-                    load_tables(blk + 1, (in_block - 2) // 2)
+                if s in (2, 4, 6):
+                    load_v(s // 2)
+                if s in (9, 12, 15, 18):
+                    load_tables(1, (s - 9) // 3)
                 sums(s - 1)
-                if blk + 1 < BLOCKS and in_block in (7, 9, 11, 13):
-                    turn_table(blk + 1, (in_block - 7) // 4, (in_block - 7) // 2 % 2)
+                if s in (15, 17, 19, 21, 23, 25, 27, 29):
+                    turn_table(1, (s - 15) // 4, (s - 15) // 2 % 2)
                 turn_q(s + 2)
                 share_q(s + 1)
                 products(s)
+                if s < 2:
+                    turn_table(0, s + 2, 0)
+                    turn_table(0, s + 2, 1)
                 regroup(s - 1)
-                if blk == 0 and in_block in (6, 8, 10, 12):
-                    group_v((in_block - 6) // 2)
+                if s in (3, 5, 7, 9):
+                    group_v((s - 3) // 2)
                 quantise(s - 2)
-                if blk == 0 and in_block in (7, 9, 11, 13):
-                    quantise_v((in_block - 7) // 2)
+                if s in (4, 6, 8, 10):
+                    quantise_v((s - 4) // 2)
                 if s % UNITS == 0:
                     multiply(s // UNITS - 2)
                     add_state(s // UNITS - 2)

@@ -28,9 +28,8 @@ ALL_UNITS = ROUNDS * UNITS
 GROUP_UNITS = HEADS * PASSES * UNITS
 TABLES = PASSES * UNITS
 LOAD_AHEAD = 3
-KEEP_UP = 92
 X = K_PASS
-XV = 320
+XV = 256
 
 
 def place(r):
@@ -197,10 +196,6 @@ def tile_attention_pb_t_kernel(tc, Q, V, state, cos, sin, out):
             for ab in range(2):
                 acc_sum = sum_psum.tile([P, PACK, P], F32, tag="sum")
                 sum_of[u].append(acc_sum)
-                if ab == 0:
-                    nc.tensor.matmul(
-                        acc_sum[:, 0, :KEEP_UP], ident[:], ident[:, :KEEP_UP], start=True, stop=True
-                    )
                 for j in range(PACK):
                     tokens = slice(j * P, (j + 1) * P)
                     nc.tensor.matmul(
@@ -282,13 +277,6 @@ def tile_attention_pb_t_kernel(tc, Q, V, state, cos, sin, out):
             )
 
         with tc.manual_schedule():
-            warm = sum_psum.tile([P, PACK, P], F32, tag="sum")
-            nc.tensor.matmul(
-                warm[:],
-                ident[:],
-                ident[:].unsqueeze(1).broadcast_to([P, PACK, P]),
-                start=True, stop=True,
-            )
             load_tables(0, 0)
             load_q(0, UNITS)
             load_tables(0, 1)

@@ -29,7 +29,7 @@ GROUP_UNITS = HEADS * PASSES * UNITS
 TABLES = PASSES * UNITS
 LOAD_AHEAD = 3
 X = K_PASS
-XV = 256
+XV = 320
 
 
 def place(r):
@@ -166,6 +166,10 @@ def tile_attention_pb_t_kernel(tc, Q, V, state, cos, sin, out):
             qs_of[u] = q_share
             nc.scalar.copy(out=q_share[:], in_=qt_of[u][:, XV:])
 
+        def for_both_tables(words, width):
+            rows = words.bitcast(BF16).rearrange("i (x ab) -> i ab x", ab=2)
+            return rows.unsqueeze(1).broadcast_to([P, 2, 2, width])
+
         def products(u):
             if u >= ALL_UNITS:
                 return
@@ -174,19 +178,18 @@ def tile_attention_pb_t_kernel(tc, Q, V, state, cos, sin, out):
             table_t = table_of[(g, c, k)]
             prod = prod_pool.tile([P, 2, 2, X], F32)
             prod_of[u] = prod
-            for engine, q_words, x0, x1 in (
-                (nc.vector, qt_of[u][:, :XV], 0, XV),
-                (nc.gpsimd, qs_of[u][:], XV, X),
-            ):
-                engine.tensor_tensor(
-                    out=prod[:, :, :, x0:x1],
-                    in0=q_words.bitcast(BF16)
-                    .rearrange("i (x ab) -> i ab x", ab=2)
-                    .unsqueeze(1)
-                    .broadcast_to([P, 2, 2, x1 - x0]),
-                    in1=table_t[:, :, :, x0:x1],
-                    op=ALU.mult,
-                )
+            nc.vector.tensor_tensor(
+                out=prod[:, :, :, :XV],
+                in0=table_t[:, :, :, :XV],
+                in1=for_both_tables(qt_of[u][:, :XV], XV),
+                op=ALU.mult,
+            )
+            nc.gpsimd.tensor_tensor(
+                out=prod[:, :, :, XV:],
+                in0=for_both_tables(qs_of[u][:], X - XV),
+                in1=table_t[:, :, :, XV:],
+                op=ALU.mult,
+            )
 
         def sums(u):
             if u < 0 or u >= ALL_UNITS:

@@ -29,7 +29,6 @@ GROUP_UNITS = HEADS * PASSES * UNITS
 TABLES = PASSES * UNITS
 LOAD_AHEAD = 3
 X = K_PASS
-XV = 320
 
 
 def place(r):
@@ -46,7 +45,6 @@ def tile_attention_pb_t_kernel(tc, Q, V, state, cos, sin, out):
         raw_pool = ctx.enter_context(tc.tile_pool(name="table_raw", bufs=TABLES))
         table_pool = ctx.enter_context(tc.tile_pool(name="tables", bufs=GROUPS * TABLES))
         q_pool = ctx.enter_context(tc.tile_pool(name="q_raw", bufs=5))
-        qs_pool = ctx.enter_context(tc.tile_pool(name="q_share", bufs=3))
         prod_pool = ctx.enter_context(tc.tile_pool(name="products", bufs=3))
         g_pool = ctx.enter_context(tc.tile_pool(name="grouped", bufs=4))
         first_pool = ctx.enter_context(tc.tile_pool(name="codes_first", bufs=3))
@@ -61,7 +59,7 @@ def tile_attention_pb_t_kernel(tc, Q, V, state, cos, sin, out):
         ident = keep.tile([P, P], F32)
         make_identity(nc, ident[:])
 
-        q_of, raw_of, table_of, qt_of, qs_of, prod_of = {}, {}, {}, {}, {}, {}
+        q_of, raw_of, table_of, qt_of, prod_of = {}, {}, {}, {}, {}
         sum_of, grouped_of, codes_of, acc_of, v_of, state_of = {}, {}, {}, {}, {}, {}
 
         def load_tables(g, i):
@@ -159,13 +157,6 @@ def tile_attention_pb_t_kernel(tc, Q, V, state, cos, sin, out):
                     ident[:],
                 )
 
-        def share_q(u):
-            if u >= ALL_UNITS:
-                return
-            q_share = qs_pool.tile([P, X - XV], F32)
-            qs_of[u] = q_share
-            nc.scalar.copy(out=q_share[:], in_=qt_of[u][:, XV:])
-
         def for_both_tables(words, width):
             rows = words.bitcast(BF16).rearrange("i (x ab) -> i ab x", ab=2)
             return rows.unsqueeze(1).broadcast_to([P, 2, 2, width])
@@ -179,15 +170,9 @@ def tile_attention_pb_t_kernel(tc, Q, V, state, cos, sin, out):
             prod = prod_pool.tile([P, 2, 2, X], F32)
             prod_of[u] = prod
             nc.vector.tensor_tensor(
-                out=prod[:, :, :, :XV],
-                in0=table_t[:, :, :, :XV],
-                in1=for_both_tables(qt_of[u][:, :XV], XV),
-                op=ALU.mult,
-            )
-            nc.gpsimd.tensor_tensor(
-                out=prod[:, :, :, XV:],
-                in0=for_both_tables(qs_of[u][:], X - XV),
-                in1=table_t[:, :, :, XV:],
+                out=prod[:],
+                in0=table_t[:],
+                in1=for_both_tables(qt_of[u][:], X),
                 op=ALU.mult,
             )
 
@@ -291,7 +276,6 @@ def tile_attention_pb_t_kernel(tc, Q, V, state, cos, sin, out):
             turn_table(0, 0, 0)
             turn_table(0, 0, 1)
             turn_q(0)
-            share_q(0)
             turn_table(0, 1, 0)
             turn_table(0, 1, 1)
             turn_q(1)
@@ -306,7 +290,6 @@ def tile_attention_pb_t_kernel(tc, Q, V, state, cos, sin, out):
                 if s in (15, 17, 19, 21, 23, 25, 27, 29):
                     turn_table(1, (s - 15) // 4, (s - 15) // 2 % 2)
                 turn_q(s + 2)
-                share_q(s + 1)
                 products(s)
                 if s < 2:
                     turn_table(0, s + 2, 0)

@@ -19,84 +19,84 @@ PACK = 4
 K_PASS = P * PACK
 PASSES = T // K_PASS
 W_UNIT = 2 * P
-UNITS = 2
-W_ROUND = UNITS * W_UNIT
-GROUPS = N // W_ROUND
-HEADS = B * NH
-ROUNDS = GROUPS * HEADS * PASSES
-ALL_UNITS = ROUNDS * UNITS
-GROUP_UNITS = HEADS * PASSES * UNITS
-TABLES = PASSES * UNITS
-LOAD_AHEAD = 3
-X = K_PASS
+UNITS = N // W_UNIT
+TURNED = UNITS - 1
+ROUNDS = B * NH * PASSES
+STEPS = ROUNDS * TURNED
+LOAD_AHEAD = 2
 
 
 def place(r):
-    rest, c = divmod(r, PASSES)
-    g, bh = divmod(rest, HEADS)
-    b, h = divmod(bh, NH)
-    return g, c, b, h
+    b, rest = divmod(r, PASSES * NH)
+    c, h = divmod(rest, NH)
+    return b, h, c
 
 
 def tile_attention_pb_t_kernel(tc, Q, V, state, cos, sin, out):
     nc = tc.nc
     with ExitStack() as ctx:
         keep = ctx.enter_context(tc.tile_pool(name="keep", bufs=1))
-        raw_pool = ctx.enter_context(tc.tile_pool(name="table_raw", bufs=TABLES))
-        table_pool = ctx.enter_context(tc.tile_pool(name="tables", bufs=GROUPS * TABLES))
-        q_pool = ctx.enter_context(tc.tile_pool(name="q_raw", bufs=5))
+        raw_pool = ctx.enter_context(tc.tile_pool(name="table_raw", bufs=4))
+        turned_pool = ctx.enter_context(tc.tile_pool(name="turned", bufs=PASSES * TURNED))
+        flat_pool = ctx.enter_context(tc.tile_pool(name="flat", bufs=PASSES))
+        q_pool = ctx.enter_context(tc.tile_pool(name="q_raw", bufs=3))
+        first_q_pool = ctx.enter_context(tc.tile_pool(name="first_q", bufs=UNITS))
+        qg_pool = ctx.enter_context(tc.tile_pool(name="q_grouped", bufs=3))
         prod_pool = ctx.enter_context(tc.tile_pool(name="products", bufs=3))
-        g_pool = ctx.enter_context(tc.tile_pool(name="grouped", bufs=4))
-        first_pool = ctx.enter_context(tc.tile_pool(name="codes_first", bufs=3))
-        last_pool = ctx.enter_context(tc.tile_pool(name="codes_last", bufs=3))
-        v_pool = ctx.enter_context(tc.tile_pool(name="v", bufs=B))
-        state_pool = ctx.enter_context(tc.tile_pool(name="state", bufs=6))
-        res_pool = ctx.enter_context(tc.tile_pool(name="res", bufs=4))
-        qt_psum = ctx.enter_context(tc.psum_pool(name="qt_psum", bufs=3))
+        flat_prod_pool = ctx.enter_context(tc.tile_pool(name="flat_products", bufs=2))
+        g_pool = ctx.enter_context(tc.tile_pool(name="grouped", bufs=3))
+        code_pool = ctx.enter_context(tc.tile_pool(name="codes", bufs=5))
+        v_pool = ctx.enter_context(tc.tile_pool(name="v", bufs=2))
+        state_pool = ctx.enter_context(tc.tile_pool(name="state", bufs=4))
+        res_pool = ctx.enter_context(tc.tile_pool(name="res", bufs=2))
+        qt_psum = ctx.enter_context(tc.psum_pool(name="qt_psum", bufs=2))
         sum_psum = ctx.enter_context(tc.psum_pool(name="sum_psum", bufs=4))
-        acc_psum = ctx.enter_context(tc.psum_pool(name="acc_psum", bufs=1))
+        acc_psum = ctx.enter_context(tc.psum_pool(name="acc_psum", bufs=2))
 
         ident = keep.tile([P, P], F32)
         make_identity(nc, ident[:])
 
-        q_of, raw_of, table_of, qt_of, prod_of = {}, {}, {}, {}, {}
+        q_of, qg_of, raw_of, table_of, qt_of, prod_of = {}, {}, {}, {}, {}, {}
         sum_of, grouped_of, codes_of, acc_of, v_of, state_of = {}, {}, {}, {}, {}, {}
 
-        def load_tables(g, i):
-            c, k = divmod(i, UNITS)
+        def load_table(c, k):
             tokens = slice(c * K_PASS, (c + 1) * K_PASS)
-            w0 = g * W_ROUND + k * W_UNIT
+            features = slice(k * W_UNIT, (k + 1) * W_UNIT)
             cos_raw = raw_pool.tile([P, PACK, W_UNIT], BF16)
             sin_raw = raw_pool.tile([P, PACK, W_UNIT], BF16)
-            raw_of[(g, c, k)] = (cos_raw, sin_raw)
+            raw_of[(c, k)] = (cos_raw, sin_raw)
             for table, table_raw in ((cos, cos_raw), (sin, sin_raw)):
                 nc.sync.dma_start(
                     out=table_raw[:],
-                    in_=table[tokens, w0 : w0 + W_UNIT].rearrange("(p j) w -> p j w", j=PACK),
+                    in_=table[tokens, features].rearrange("(p j) w -> p j w", j=PACK),
                 )
 
-        def load_q(r, split):
+        def load_q(r, k0, k1):
             if r >= ROUNDS:
                 return
-            g, c, b, h = place(r)
-            tokens = slice(c * K_PASS, (c + 1) * K_PASS)
-            q_raw = q_pool.tile([P, PACK, W_ROUND], BF16)
-            q_of[r] = q_raw
-            width = W_ROUND // split
-            for i in range(split):
-                w0 = g * W_ROUND + i * width
-                nc.sync.dma_start(
-                    out=q_raw[:, :, i * width : (i + 1) * width],
-                    in_=Q[b, h, tokens, w0 : w0 + width].rearrange("(p j) w -> p j w", j=PACK),
-                )
+            b, h, c = place(r)
+            q_raw = (first_q_pool if r == 0 else q_pool).tile(
+                [P, PACK, (k1 - k0) * W_UNIT], BF16, name="q_raw"
+            )
+            for k in range(k0, k1):
+                q_of[(r, k)] = q_raw[:, :, (k - k0) * W_UNIT : (k - k0 + 1) * W_UNIT]
+            nc.sync.dma_start(
+                out=q_raw[:],
+                in_=Q[
+                    b, h, c * K_PASS : (c + 1) * K_PASS, k0 * W_UNIT : k1 * W_UNIT
+                ].rearrange("(p j) w -> p j w", j=PACK),
+            )
+
+        def load_state(r):
+            if r >= ROUNDS:
+                return
+            b, h, c = place(r)
             if c == PASSES - 1:
                 state_sb = state_pool.tile([P, UNITS, 2, D], BF16)
                 state_of[r] = state_sb
                 nc.sync.dma_start(
                     out=state_sb[:],
-                    in_=state[b, h, g * W_ROUND : (g + 1) * W_ROUND, :].rearrange(
-                        "(k i ab) d -> i k ab d", k=UNITS, ab=2
-                    ),
+                    in_=state[b, h].rearrange("(k i ab) d -> i k ab d", k=UNITS, ab=2),
                 )
 
         def load_v(b):
@@ -121,69 +121,117 @@ def tile_attention_pb_t_kernel(tc, Q, V, state, cos, sin, out):
             )
             v_of[b] = (v_codes, v_scales)
 
-        def turn_table(g, i, which):
-            key = (g, *divmod(i, UNITS))
-            if which == 0:
-                table_t = table_pool.tile([P, 2, 2, X], BF16)
-                table_of[key] = table_t
-            table_t = table_of[key]
-            table_raw = raw_of[key][which]
-            bank = sum_psum.tile([P, PACK, P], F32, tag="sum")
-            for j in range(PACK):
-                nc.tensor.transpose(bank[:, j, :], table_raw[:, j, :].bitcast(F32), ident[:])
-            by_parity = (
-                bank[:].rearrange("i j p -> i (j p)").bitcast(BF16)
-                .rearrange("i (x ab) -> i ab x", ab=2)
-            )
-            if which == 0:
-                if g == 0:
-                    nc.vector.tensor_copy(out=table_t[:, 0], in_=by_parity)
+        def turn_table(c, k):
+            table_t = turned_pool.tile([P, 2, 2, K_PASS], BF16)
+            table_of[(c, k)] = table_t
+            for which in range(2):
+                bank = sum_psum.tile([P, PACK, P], F32, tag="sum")
+                for j in range(PACK):
+                    nc.tensor.transpose(
+                        bank[:, j, :], raw_of[(c, k)][which][:, j, :].bitcast(F32), ident[:]
+                    )
+                by_parity = (
+                    bank[:].rearrange("i j p -> i (j p)").bitcast(BF16)
+                    .rearrange("i (x ab) -> i ab x", ab=2)
+                )
+                if which == 0:
+                    if c == 0:
+                        nc.vector.tensor_copy(out=table_t[:, 0], in_=by_parity)
+                    else:
+                        nc.scalar.copy(out=table_t[:, 0], in_=by_parity)
                 else:
-                    nc.scalar.copy(out=table_t[:, 0], in_=by_parity)
-            else:
-                nc.scalar.copy(out=table_t[:, 1, 0, :], in_=by_parity[:, 1])
-                nc.scalar.mul(out=table_t[:, 1, 1, :], in_=by_parity[:, 0], mul=-1.0)
+                    nc.scalar.copy(out=table_t[:, 1, 0, :], in_=by_parity[:, 1])
+                    nc.scalar.mul(out=table_t[:, 1, 1, :], in_=by_parity[:, 0], mul=-1.0)
 
-        def turn_q(u):
-            if u >= ALL_UNITS:
+        def group_table(c):
+            table_g = flat_pool.tile([P, 2, 2, P, PACK], BF16)
+            table_of[(c, TURNED)] = table_g
+            for which in range(2):
+                by_parity = raw_of[(c, TURNED)][which][:].rearrange("p j (i ab) -> p ab i j", ab=2)
+                if c == 0:
+                    nc.gpsimd.tensor_copy(out=table_g[:, which], in_=by_parity)
+                else:
+                    nc.scalar.copy(out=table_g[:, which], in_=by_parity)
+
+        def group_q(r):
+            if r >= ROUNDS:
                 return
-            r, k = divmod(u, UNITS)
-            qt = qt_psum.tile([P, X], F32)
-            qt_of[u] = qt
+            q_grouped = qg_pool.tile([P, 2, P, PACK], BF16)
+            qg_of[r] = q_grouped
+            nc.scalar.copy(
+                out=q_grouped[:],
+                in_=q_of[(r, TURNED)].rearrange("p j (i ab) -> p ab i j", ab=2),
+            )
+
+        def turn_q(n):
+            if n >= STEPS:
+                return
+            r, k = divmod(n, TURNED)
+            qt = qt_psum.tile([P, K_PASS], F32)
+            qt_of[n] = qt
             for j in range(PACK):
                 nc.tensor.transpose(
                     qt[:, j * P : (j + 1) * P],
-                    q_of[r][:, j, k * W_UNIT : (k + 1) * W_UNIT].bitcast(F32),
+                    q_of[(r, k)][:, j, :].bitcast(F32),
                     ident[:],
                 )
 
-        def for_both_tables(words, width):
-            rows = words.bitcast(BF16).rearrange("i (x ab) -> i ab x", ab=2)
-            return rows.unsqueeze(1).broadcast_to([P, 2, 2, width])
-
-        def products(u):
-            if u >= ALL_UNITS:
+        def products(n):
+            if n >= STEPS:
                 return
-            r, k = divmod(u, UNITS)
-            g, c, b, h = place(r)
-            table_t = table_of[(g, c, k)]
-            prod = prod_pool.tile([P, 2, 2, X], F32)
-            prod_of[u] = prod
+            r, k = divmod(n, TURNED)
+            prod = prod_pool.tile([P, 2, 2, K_PASS], F32)
+            prod_of[n] = prod
+            q_rows = qt_of[n][:].bitcast(BF16).rearrange("i (x ab) -> i ab x", ab=2)
             nc.vector.tensor_tensor(
                 out=prod[:],
-                in0=table_t[:],
-                in1=for_both_tables(qt_of[u][:], X),
+                in0=q_rows.unsqueeze(1).broadcast_to([P, 2, 2, K_PASS]),
+                in1=table_of[(place(r)[2], k)][:],
                 op=ALU.mult,
             )
 
-        def sums(u):
-            if u < 0 or u >= ALL_UNITS:
+        def grouped_tile(r):
+            if r not in grouped_of:
+                grouped = g_pool.tile([P, UNITS, 2, P, PACK], BF16, align_bytes=64)
+                grouped_of[r] = grouped
+            return grouped_of[r]
+
+        def rope_flat(r):
+            if r >= ROUNDS:
                 return
-            prod = prod_of[u]
-            sum_of[u] = []
+            table_g = table_of[(place(r)[2], TURNED)]
+            flat = flat_prod_pool.tile([P, 2, 2, P, PACK], F32)
+            grouped = grouped_tile(r)
+
+            def product(which, ab):
+                nc.gpsimd.tensor_tensor(
+                    out=flat[:, which, ab],
+                    in0=qg_of[r][:, ab if which == 0 else 1 - ab],
+                    in1=table_g[:, which, ab],
+                    op=ALU.mult,
+                )
+
+            def combine(ab):
+                nc.gpsimd.tensor_tensor(
+                    out=grouped[:, TURNED, ab], in0=flat[:, 0, ab], in1=flat[:, 1, ab],
+                    op=ALU.subtract if ab == 0 else ALU.add,
+                )
+
+            product(0, 0)
+            product(1, 0)
+            product(0, 1)
+            combine(0)
+            product(1, 1)
+            combine(1)
+
+        def sums(n):
+            if n < 0 or n >= STEPS:
+                return
+            prod = prod_of[n]
+            sum_of[n] = []
             for ab in range(2):
                 acc_sum = sum_psum.tile([P, PACK, P], F32, tag="sum")
-                sum_of[u].append(acc_sum)
+                sum_of[n].append(acc_sum)
                 for j in range(PACK):
                     tokens = slice(j * P, (j + 1) * P)
                     nc.tensor.matmul(
@@ -195,111 +243,120 @@ def tile_attention_pb_t_kernel(tc, Q, V, state, cos, sin, out):
                         start=False, stop=True, is_transpose=True,
                     )
 
-        def regroup(u):
-            if u < 0 or u >= ALL_UNITS:
+        def regroup(n):
+            if n < 0 or n >= STEPS:
                 return
-            grouped = g_pool.tile([P, 2, P, PACK], BF16, align_bytes=64)
-            grouped_of[u] = grouped
+            r, k = divmod(n, TURNED)
+            grouped = grouped_tile(r)
             for ab in range(2):
                 nc.scalar.copy(
-                    out=grouped[:, ab], in_=sum_of[u][ab][:].rearrange("p j i -> p i j")
+                    out=grouped[:, k, ab], in_=sum_of[n][ab][:].rearrange("p j i -> p i j")
                 )
 
-        def quantise(u):
-            if u < 0 or u >= ALL_UNITS:
+        def quantise(r):
+            if r < 0 or r >= ROUNDS:
                 return
-            r, k = divmod(u, UNITS)
-            g, c, b, h = place(r)
-            key = (g, c, b, h)
-            if k == 0:
-                pool = first_pool if c == 0 else last_pool
-                codes = pool.tile([P, UNITS, 2, P], U32, align_bytes=64)
-                scales = pool.tile([P, UNITS, 2, P], U8, align_bytes=64)
-                codes_of[key] = (codes, scales)
-            codes, scales = codes_of[key]
+            codes = code_pool.tile([P, UNITS, 2, P], U32, align_bytes=64)
+            scales = code_pool.tile([P, UNITS, 2, P], U8, align_bytes=64)
+            codes_of[r] = (codes, scales)
             nc.vector.quantize_mx(
-                out=codes[:, k].rearrange("p ab i -> p (ab i)").bitcast(FP8X4),
-                scales=scales[:, k].rearrange("p ab i -> p (ab i)"),
-                in_=grouped_of[u][:].rearrange("p ab i j -> p (ab i j)"),
+                out=codes[:].rearrange("p k ab i -> p (k ab i)").bitcast(FP8X4),
+                scales=scales[:].rearrange("p k ab i -> p (k ab i)"),
+                in_=grouped_of[r][:].rearrange("p k ab i j -> p (k ab i j)"),
             )
 
         def multiply(r):
-            if r < 0 or r >= ROUNDS or place(r)[1] != PASSES - 1:
+            if r < 0 or r >= ROUNDS or place(r)[2] != PASSES - 1:
                 return
-            g, c, b, h = place(r)
+            b, h, c = place(r)
             v_codes, v_scales = v_of[b]
-            acc = acc_psum.tile([P, UNITS, 2, D], F32)
-            acc_of[r] = acc
-            for k in range(UNITS):
-                for ab in range(2):
-                    for t in range(PASSES):
-                        codes, scales = codes_of[(g, t, b, h)]
-                        nc.tensor.matmul_mx(
-                            out=acc[:, k, ab, :],
-                            lhsT=codes[:, k, ab, :].bitcast(FP8X4),
-                            lhsT_scale=scales[:, k, ab, :],
-                            rhs=v_codes[:, t, :].bitcast(FP8X4),
-                            rhs_scale=v_scales[:, t, :],
-                            start=(t == 0),
-                            stop=(t == PASSES - 1),
-                        )
+            acc_of[r] = []
+            for half in range(2):
+                acc = acc_psum.tile([P, UNITS // 2, 2, D], F32)
+                acc_of[r].append(acc)
+                for k in range(UNITS // 2):
+                    for ab in range(2):
+                        for t in range(PASSES):
+                            codes, scales = codes_of[r - (PASSES - 1 - t) * NH]
+                            unit = half * (UNITS // 2) + k
+                            nc.tensor.matmul_mx(
+                                out=acc[:, k, ab, :],
+                                lhsT=codes[:, unit, ab, :].bitcast(FP8X4),
+                                lhsT_scale=scales[:, unit, ab, :],
+                                rhs=v_codes[:, t, :].bitcast(FP8X4),
+                                rhs_scale=v_scales[:, t, :],
+                                start=(t == 0),
+                                stop=(t == PASSES - 1),
+                            )
 
         def add_state(r):
-            if r < 0 or r >= ROUNDS or place(r)[1] != PASSES - 1:
+            if r < 0 or r >= ROUNDS or place(r)[2] != PASSES - 1:
                 return
-            g, c, b, h = place(r)
+            b, h, c = place(r)
             res = res_pool.tile([P, UNITS, 2, D], F32)
-            nc.vector.scalar_tensor_tensor(
-                out=res[:],
-                in0=acc_of[r][:],
-                scalar=SCALE,
-                in1=state_of[r][:],
-                op0=ALU.mult,
-                op1=ALU.add,
-            )
-            nc.sync.dma_start(
-                out=out[b, h, g * W_ROUND : (g + 1) * W_ROUND, :].rearrange(
-                    "(k i ab) d -> i k ab d", k=UNITS, ab=2
-                ),
-                in_=res[:],
-            )
+            for half in range(2):
+                units = slice(half * (UNITS // 2), (half + 1) * (UNITS // 2))
+                nc.vector.scalar_tensor_tensor(
+                    out=res[:, units],
+                    in0=acc_of[r][half][:],
+                    scalar=SCALE,
+                    in1=state_of[r][:, units],
+                    op0=ALU.mult,
+                    op1=ALU.add,
+                )
+                nc.sync.dma_start(
+                    out=out[b, h].rearrange("(k i ab) d -> i k ab d", k=UNITS, ab=2)[:, units],
+                    in_=res[:, units],
+                )
 
         with tc.manual_schedule():
-            load_tables(0, 0)
-            load_q(0, UNITS)
-            load_tables(0, 1)
-            load_q(1, 1)
+            load_table(0, 0)
+            load_q(0, 0, 1)
+            load_table(0, 3)
+            load_q(0, 3, 4)
+            load_table(0, 1)
+            load_q(0, 1, 2)
+            load_table(0, 2)
+            load_q(0, 2, 3)
+            load_q(1, 0, UNITS)
+            load_table(1, 3)
+            for k in range(TURNED):
+                load_table(1, k)
             load_v(0)
-            load_tables(0, 2)
-            load_tables(0, 3)
-            load_q(2, 1)
-            turn_table(0, 0, 0)
-            turn_table(0, 0, 1)
+            turn_table(0, 0)
             turn_q(0)
-            turn_table(0, 1, 0)
-            turn_table(0, 1, 1)
+            group_table(0)
+            group_q(0)
             turn_q(1)
-            for s in range(ALL_UNITS + 6):
-                if s % UNITS == 0:
-                    load_q(s // UNITS + LOAD_AHEAD, 1)
-                if s in (2, 4, 6):
-                    load_v(s // 2)
-                if s in (9, 12, 15, 18):
-                    load_tables(1, (s - 9) // 3)
-                sums(s - 1)
-                if s in (15, 17, 19, 21, 23, 25, 27, 29):
-                    turn_table(1, (s - 15) // 4, (s - 15) // 2 % 2)
-                turn_q(s + 2)
-                products(s)
-                if s < 2:
-                    turn_table(0, s + 2, 0)
-                    turn_table(0, s + 2, 1)
-                regroup(s - 1)
-                if s in (3, 5, 7, 9):
-                    group_v((s - 3) // 2)
-                quantise(s - 2)
-                if s in (4, 6, 8, 10):
-                    quantise_v((s - 4) // 2)
-                if s % UNITS == 0:
-                    multiply(s // UNITS - 2)
-                    add_state(s // UNITS - 2)
+            for n in range(STEPS + 3 * TURNED):
+                r, k = divmod(n, TURNED)
+                if k == 0:
+                    load_q(r + LOAD_AHEAD, 0, UNITS)
+                    load_state(r + LOAD_AHEAD)
+                b_next, rest = divmod(n, TURNED * PASSES * NH)
+                if rest == 6 and b_next + 1 < B:
+                    load_v(b_next + 1)
+                if k == 2:
+                    multiply(r - 1)
+                sums(n - 1)
+                turn_q(n + 2)
+                if k == 0:
+                    rope_flat(r)
+                products(n)
+                if n + 1 < TURNED:
+                    turn_table(0, n + 1)
+                elif n in (3, 4, 5):
+                    turn_table(1, n - 3)
+                regroup(n - 1)
+                if n == 2:
+                    group_table(1)
+                if k == 0:
+                    group_q(r + 1)
+                if k == 1:
+                    quantise(r - 1)
+                if rest == 7 and b_next < B:
+                    group_v(b_next)
+                if rest == 8 and b_next < B:
+                    quantise_v(b_next)
+                if k == 2:
+                    add_state(r - 1)

@@ -21,31 +21,44 @@ PASSES = T // K_PASS
 W_UNIT = 2 * P
 UNITS = N // W_UNIT
 TURNED = UNITS - 1
-ROUNDS = B * NH * PASSES
-STEPS = ROUNDS * TURNED
-LOAD_AHEAD = 2
+PAIRS = [(0, 0), (1, 0), (0, 1), (1, 1), (2, 1), (2, 0), (3, 0), (3, 1)]
+ROUNDS = NH * len(PAIRS)
+PER_PAIR = NH * TURNED
+STEPS = PER_PAIR * len(PAIRS)
 
 
 def place(r):
-    b, rest = divmod(r, PASSES * NH)
-    c, h = divmod(rest, NH)
+    p, h = divmod(r, NH)
+    b, c = PAIRS[p]
     return b, h, c
+
+
+def step(n):
+    p, rest = divmod(n, PER_PAIR)
+    if p == len(PAIRS) - 1:
+        h, k = divmod(rest, TURNED)
+    else:
+        k, h = divmod(rest, NH)
+    return p * NH + h, k
+
+
+def last_of_batch(p):
+    return PAIRS[p][0] in [b for b, c in PAIRS[:p]]
 
 
 def tile_attention_pb_t_kernel(tc, Q, V, state, cos, sin, out):
     nc = tc.nc
     with ExitStack() as ctx:
         keep = ctx.enter_context(tc.tile_pool(name="keep", bufs=1))
-        raw_pool = ctx.enter_context(tc.tile_pool(name="table_raw", bufs=4))
+        raw_pool = ctx.enter_context(tc.tile_pool(name="table_raw", bufs=6))
         turned_pool = ctx.enter_context(tc.tile_pool(name="turned", bufs=PASSES * TURNED))
         flat_pool = ctx.enter_context(tc.tile_pool(name="flat", bufs=PASSES))
-        q_pool = ctx.enter_context(tc.tile_pool(name="q_raw", bufs=3))
-        first_q_pool = ctx.enter_context(tc.tile_pool(name="first_q", bufs=UNITS))
+        q_pool = ctx.enter_context(tc.tile_pool(name="q_raw", bufs=5))
+        first_q_pool = ctx.enter_context(tc.tile_pool(name="first_q", bufs=6))
         qg_pool = ctx.enter_context(tc.tile_pool(name="q_grouped", bufs=3))
         prod_pool = ctx.enter_context(tc.tile_pool(name="products", bufs=3))
-        flat_prod_pool = ctx.enter_context(tc.tile_pool(name="flat_products", bufs=2))
-        g_pool = ctx.enter_context(tc.tile_pool(name="grouped", bufs=3))
-        code_pool = ctx.enter_context(tc.tile_pool(name="codes", bufs=5))
+        g_pool = ctx.enter_context(tc.tile_pool(name="grouped", bufs=5))
+        code_pool = ctx.enter_context(tc.tile_pool(name="codes", bufs=7))
         v_pool = ctx.enter_context(tc.tile_pool(name="v", bufs=2))
         state_pool = ctx.enter_context(tc.tile_pool(name="state", bufs=4))
         res_pool = ctx.enter_context(tc.tile_pool(name="res", bufs=2))
@@ -56,26 +69,29 @@ def tile_attention_pb_t_kernel(tc, Q, V, state, cos, sin, out):
         ident = keep.tile([P, P], F32)
         make_identity(nc, ident[:])
 
-        q_of, qg_of, raw_of, table_of, qt_of, prod_of = {}, {}, {}, {}, {}, {}
-        sum_of, grouped_of, codes_of, acc_of, v_of, state_of = {}, {}, {}, {}, {}, {}
+        q_of, qg_of, raw_of, bank_of, table_of, qt_of, prod_of = {}, {}, {}, {}, {}, {}, {}
+        flat_of, sum_of, grouped_of, codes_of, acc_of, v_of, state_of, res_of = {}, {}, {}, {}, {}, {}, {}, {}
 
-        def load_table(c, k):
+        def load_table(c, k0, k1):
             tokens = slice(c * K_PASS, (c + 1) * K_PASS)
-            features = slice(k * W_UNIT, (k + 1) * W_UNIT)
-            cos_raw = raw_pool.tile([P, PACK, W_UNIT], BF16)
-            sin_raw = raw_pool.tile([P, PACK, W_UNIT], BF16)
-            raw_of[(c, k)] = (cos_raw, sin_raw)
-            for table, table_raw in ((cos, cos_raw), (sin, sin_raw)):
+            for k in range(k0, k1):
+                raw_of[(c, k)] = []
+            for table in (cos, sin):
+                table_raw = (raw_pool if c == 0 else q_pool).tile(
+                    [P, PACK, (k1 - k0) * W_UNIT], BF16, name="table_raw" if c == 0 else "q_raw"
+                )
+                for k in range(k0, k1):
+                    raw_of[(c, k)].append(table_raw[:, :, (k - k0) * W_UNIT : (k - k0 + 1) * W_UNIT])
                 nc.sync.dma_start(
                     out=table_raw[:],
-                    in_=table[tokens, features].rearrange("(p j) w -> p j w", j=PACK),
+                    in_=table[tokens, k0 * W_UNIT : k1 * W_UNIT].rearrange("(p j) w -> p j w", j=PACK),
                 )
 
         def load_q(r, k0, k1):
             if r >= ROUNDS:
                 return
             b, h, c = place(r)
-            q_raw = (first_q_pool if r == 0 else q_pool).tile(
+            q_raw = (first_q_pool if r < NH else q_pool).tile(
                 [P, PACK, (k1 - k0) * W_UNIT], BF16, name="q_raw"
             )
             for k in range(k0, k1):
@@ -88,16 +104,13 @@ def tile_attention_pb_t_kernel(tc, Q, V, state, cos, sin, out):
             )
 
         def load_state(r):
-            if r >= ROUNDS:
-                return
             b, h, c = place(r)
-            if c == PASSES - 1:
-                state_sb = state_pool.tile([P, UNITS, 2, D], BF16)
-                state_of[r] = state_sb
-                nc.sync.dma_start(
-                    out=state_sb[:],
-                    in_=state[b, h].rearrange("(k i ab) d -> i k ab d", k=UNITS, ab=2),
-                )
+            state_sb = state_pool.tile([P, UNITS, 2, D], BF16)
+            state_of[r] = state_sb
+            nc.sync.dma_start(
+                out=state_sb[:],
+                in_=state[b, h].rearrange("(k i ab) d -> i k ab d", k=UNITS, ab=2),
+            )
 
         def load_v(b):
             v_raw = v_pool.tile([P, PASSES, PACK, D], BF16)
@@ -122,36 +135,38 @@ def tile_attention_pb_t_kernel(tc, Q, V, state, cos, sin, out):
             v_of[b] = (v_codes, v_scales)
 
         def turn_table(c, k):
-            table_t = turned_pool.tile([P, 2, 2, K_PASS], BF16)
-            table_of[(c, k)] = table_t
+            bank_of[(c, k)] = []
             for which in range(2):
                 bank = sum_psum.tile([P, PACK, P], F32, tag="sum")
                 for j in range(PACK):
                     nc.tensor.transpose(
                         bank[:, j, :], raw_of[(c, k)][which][:, j, :].bitcast(F32), ident[:]
                     )
-                by_parity = (
+                bank_of[(c, k)].append(
                     bank[:].rearrange("i j p -> i (j p)").bitcast(BF16)
                     .rearrange("i (x ab) -> i ab x", ab=2)
                 )
-                if which == 0:
-                    if c == 0:
-                        nc.vector.tensor_copy(out=table_t[:, 0], in_=by_parity)
-                    else:
-                        nc.scalar.copy(out=table_t[:, 0], in_=by_parity)
-                else:
-                    nc.scalar.copy(out=table_t[:, 1, 0, :], in_=by_parity[:, 1])
-                    nc.scalar.mul(out=table_t[:, 1, 1, :], in_=by_parity[:, 0], mul=-1.0)
 
-        def group_table(c):
-            table_g = flat_pool.tile([P, 2, 2, P, PACK], BF16)
-            table_of[(c, TURNED)] = table_g
-            for which in range(2):
-                by_parity = raw_of[(c, TURNED)][which][:].rearrange("p j (i ab) -> p ab i j", ab=2)
-                if c == 0:
-                    nc.gpsimd.tensor_copy(out=table_g[:, which], in_=by_parity)
-                else:
-                    nc.scalar.copy(out=table_g[:, which], in_=by_parity)
+        def keep_cos(c, k):
+            table_t = turned_pool.tile([P, 2, 2, K_PASS], BF16)
+            table_of[(c, k)] = table_t
+            if c == 0:
+                nc.vector.tensor_copy(out=table_t[:, 0], in_=bank_of[(c, k)][0])
+            else:
+                nc.scalar.copy(out=table_t[:, 0], in_=bank_of[(c, k)][0])
+
+        def keep_sin(c, k):
+            table_t = table_of[(c, k)]
+            by_parity = bank_of[(c, k)][1]
+            nc.scalar.copy(out=table_t[:, 1, 0, :], in_=by_parity[:, 1])
+            nc.scalar.mul(out=table_t[:, 1, 1, :], in_=by_parity[:, 0], mul=-1.0)
+
+        def group_table(c, which):
+            if (c, TURNED) not in table_of:
+                table_g = flat_pool.tile([P, 2, 2, P, PACK], BF16)
+                table_of[(c, TURNED)] = table_g
+            by_parity = raw_of[(c, TURNED)][which].rearrange("p j (i ab) -> p ab i j", ab=2)
+            nc.scalar.copy(out=table_of[(c, TURNED)][:, which], in_=by_parity)
 
         def group_q(r):
             if r >= ROUNDS:
@@ -166,7 +181,7 @@ def tile_attention_pb_t_kernel(tc, Q, V, state, cos, sin, out):
         def turn_q(n):
             if n >= STEPS:
                 return
-            r, k = divmod(n, TURNED)
+            r, k = step(n)
             qt = qt_psum.tile([P, K_PASS], F32)
             qt_of[n] = qt
             for j in range(PACK):
@@ -179,7 +194,7 @@ def tile_attention_pb_t_kernel(tc, Q, V, state, cos, sin, out):
         def products(n):
             if n >= STEPS:
                 return
-            r, k = divmod(n, TURNED)
+            r, k = step(n)
             prod = prod_pool.tile([P, 2, 2, K_PASS], F32)
             prod_of[n] = prod
             q_rows = qt_of[n][:].bitcast(BF16).rearrange("i (x ab) -> i ab x", ab=2)
@@ -192,33 +207,38 @@ def tile_attention_pb_t_kernel(tc, Q, V, state, cos, sin, out):
 
         def grouped_tile(r):
             if r not in grouped_of:
-                grouped = g_pool.tile([P, UNITS, 2, P, PACK], BF16, align_bytes=64)
+                grouped = g_pool.tile([P, UNITS, 2, P, PACK], BF16, align_bytes=64, tag="g")
                 grouped_of[r] = grouped
+                flat = g_pool.tile([P, 2, 2, P, PACK], F32, align_bytes=64, tag="g")
+                flat_of[r] = flat
             return grouped_of[r]
 
         def rope_flat(r):
             if r >= ROUNDS:
                 return
             table_g = table_of[(place(r)[2], TURNED)]
-            flat = flat_prod_pool.tile([P, 2, 2, P, PACK], F32)
             grouped = grouped_tile(r)
+            flat = flat_of[r]
 
-            def product(which, ab):
-                nc.gpsimd.tensor_tensor(
+            def product(which, ab, engine=nc.gpsimd):
+                engine.tensor_tensor(
                     out=flat[:, which, ab],
                     in0=qg_of[r][:, ab if which == 0 else 1 - ab],
                     in1=table_g[:, which, ab],
                     op=ALU.mult,
                 )
 
-            def combine(ab):
-                nc.gpsimd.tensor_tensor(
+            def combine(ab, engine=nc.gpsimd):
+                engine.tensor_tensor(
                     out=grouped[:, TURNED, ab], in0=flat[:, 0, ab], in1=flat[:, 1, ab],
                     op=ALU.subtract if ab == 0 else ALU.add,
                 )
 
             product(0, 0)
             product(1, 0)
+            if r == ROUNDS - 1:
+                combine(0)
+                return product, combine
             product(0, 1)
             combine(0)
             product(1, 1)
@@ -246,117 +266,175 @@ def tile_attention_pb_t_kernel(tc, Q, V, state, cos, sin, out):
         def regroup(n):
             if n < 0 or n >= STEPS:
                 return
-            r, k = divmod(n, TURNED)
+            r, k = step(n)
             grouped = grouped_tile(r)
             for ab in range(2):
                 nc.scalar.copy(
                     out=grouped[:, k, ab], in_=sum_of[n][ab][:].rearrange("p j i -> p i j")
                 )
 
-        def quantise(r):
-            if r < 0 or r >= ROUNDS:
-                return
-            codes = code_pool.tile([P, UNITS, 2, P], U32, align_bytes=64)
-            scales = code_pool.tile([P, UNITS, 2, P], U8, align_bytes=64)
-            codes_of[r] = (codes, scales)
+        def quantise(r, part=0, parts=1):
+            if part == 0:
+                codes = code_pool.tile([P, UNITS, 2, P], U32, align_bytes=64)
+                scales = code_pool.tile([P, UNITS, 2, P], U8, align_bytes=64)
+                codes_of[r] = (codes, scales)
+            codes, scales = codes_of[r]
+            units = slice(part * UNITS // parts, (part + 1) * UNITS // parts)
             nc.vector.quantize_mx(
-                out=codes[:].rearrange("p k ab i -> p (k ab i)").bitcast(FP8X4),
-                scales=scales[:].rearrange("p k ab i -> p (k ab i)"),
-                in_=grouped_of[r][:].rearrange("p k ab i j -> p (k ab i j)"),
+                out=codes[:, units].rearrange("p k ab i -> p (k ab i)").bitcast(FP8X4),
+                scales=scales[:, units].rearrange("p k ab i -> p (k ab i)"),
+                in_=grouped_of[r][:, units].rearrange("p k ab i j -> p (k ab i j)"),
             )
 
-        def multiply(r):
-            if r < 0 or r >= ROUNDS or place(r)[2] != PASSES - 1:
-                return
+        def multiply(r, half):
             b, h, c = place(r)
             v_codes, v_scales = v_of[b]
-            acc_of[r] = []
-            for half in range(2):
-                acc = acc_psum.tile([P, UNITS // 2, 2, D], F32)
-                acc_of[r].append(acc)
-                for k in range(UNITS // 2):
-                    for ab in range(2):
-                        for t in range(PASSES):
-                            codes, scales = codes_of[r - (PASSES - 1 - t) * NH]
-                            unit = half * (UNITS // 2) + k
-                            nc.tensor.matmul_mx(
-                                out=acc[:, k, ab, :],
-                                lhsT=codes[:, unit, ab, :].bitcast(FP8X4),
-                                lhsT_scale=scales[:, unit, ab, :],
-                                rhs=v_codes[:, t, :].bitcast(FP8X4),
-                                rhs_scale=v_scales[:, t, :],
-                                start=(t == 0),
-                                stop=(t == PASSES - 1),
-                            )
+            acc = acc_psum.tile([P, UNITS // 2, 2, D], F32)
+            acc_of[(r, half)] = acc
+            rounds = [s for s in range(r + 1) if place(s)[:2] == (b, h)]
+            for k in range(UNITS // 2):
+                unit = half * (UNITS // 2) + k
+                for ab in range(2):
+                    for s in rounds:
+                        codes, scales = codes_of[s]
+                        t = place(s)[2]
+                        nc.tensor.matmul_mx(
+                            out=acc[:, k, ab, :],
+                            lhsT=codes[:, unit, ab, :].bitcast(FP8X4),
+                            lhsT_scale=scales[:, unit, ab, :],
+                            rhs=v_codes[:, t, :].bitcast(FP8X4),
+                            rhs_scale=v_scales[:, t, :],
+                            start=(s == rounds[0]),
+                            stop=(s == rounds[-1]),
+                        )
 
-        def add_state(r):
-            if r < 0 or r >= ROUNDS or place(r)[2] != PASSES - 1:
-                return
+        def add_state(r, half):
             b, h, c = place(r)
-            res = res_pool.tile([P, UNITS, 2, D], F32)
-            for half in range(2):
-                units = slice(half * (UNITS // 2), (half + 1) * (UNITS // 2))
-                nc.vector.scalar_tensor_tensor(
-                    out=res[:, units],
-                    in0=acc_of[r][half][:],
-                    scalar=SCALE,
-                    in1=state_of[r][:, units],
-                    op0=ALU.mult,
-                    op1=ALU.add,
-                )
-                nc.sync.dma_start(
-                    out=out[b, h].rearrange("(k i ab) d -> i k ab d", k=UNITS, ab=2)[:, units],
-                    in_=res[:, units],
-                )
+            if half == 0:
+                res = res_pool.tile([P, UNITS, 2, D], F32)
+                res_of[r] = res
+            res = res_of[r]
+            units = slice(half * (UNITS // 2), (half + 1) * (UNITS // 2))
+            nc.vector.scalar_tensor_tensor(
+                out=res[:, units],
+                in0=acc_of[(r, half)][:],
+                scalar=SCALE,
+                in1=state_of[r][:, units],
+                op0=ALU.mult,
+                op1=ALU.add,
+            )
+            nc.sync.dma_start(
+                out=out[b, h].rearrange("(k i ab) d -> i k ab d", k=UNITS, ab=2)[:, units],
+                in_=res[:, units],
+            )
 
         with tc.manual_schedule():
-            load_table(0, 0)
+            load_table(0, 0, 1)
             load_q(0, 0, 1)
-            load_table(0, 3)
-            load_q(0, 3, 4)
-            load_table(0, 1)
+            load_q(1, 0, 1)
+            load_table(0, TURNED, UNITS)
+            load_q(0, TURNED, UNITS)
+            load_table(0, 1, 2)
             load_q(0, 1, 2)
-            load_table(0, 2)
+            load_q(1, 1, 2)
+            load_table(0, 2, 3)
             load_q(0, 2, 3)
-            load_q(1, 0, UNITS)
-            load_table(1, 3)
-            for k in range(TURNED):
-                load_table(1, k)
-            load_v(0)
+            load_q(1, 2, 3)
+            load_q(1, TURNED, UNITS)
+            load_q(2, 0, UNITS)
+            load_q(3, 0, UNITS)
+            load_table(1, 0, UNITS)
             turn_table(0, 0)
+            keep_cos(0, 0)
+            keep_sin(0, 0)
             turn_q(0)
-            group_table(0)
-            group_q(0)
             turn_q(1)
-            for n in range(STEPS + 3 * TURNED):
-                r, k = divmod(n, TURNED)
-                if k == 0:
-                    load_q(r + LOAD_AHEAD, 0, UNITS)
-                    load_state(r + LOAD_AHEAD)
-                b_next, rest = divmod(n, TURNED * PASSES * NH)
-                if rest == 6 and b_next + 1 < B:
-                    load_v(b_next + 1)
-                if k == 2:
-                    multiply(r - 1)
+            turn_table(0, 1)
+            group_table(0, 0)
+            group_table(0, 1)
+            group_q(0)
+            rope_flat(0)
+            for n in range(STEPS):
+                p, at = divmod(n, PER_PAIR)
+                first = NH * p
+                done = first - NH
+                batch_done = 0 < p and last_of_batch(p - 1)
+                if at == 0 and 1 < p + 1 < len(PAIRS):
+                    load_q(first + 2, 0, UNITS)
+                    load_q(first + 3, 0, UNITS)
+                if at == 1 and p < len(PAIRS) and last_of_batch(p):
+                    load_state(first)
+                    load_state(first + 1)
+                    load_v(PAIRS[p][0])
+
                 sums(n - 1)
-                turn_q(n + 2)
-                if k == 0:
-                    rope_flat(r)
-                products(n)
-                if n + 1 < TURNED:
-                    turn_table(0, n + 1)
-                elif n in (3, 4, 5):
-                    turn_table(1, n - 3)
-                regroup(n - 1)
                 if n == 2:
-                    group_table(1)
-                if k == 0:
-                    group_q(r + 1)
-                if k == 1:
-                    quantise(r - 1)
-                if rest == 7 and b_next < B:
-                    group_v(b_next)
-                if rest == 8 and b_next < B:
-                    quantise_v(b_next)
-                if k == 2:
-                    add_state(r - 1)
+                    turn_table(0, 2)
+                if n in (6, 8, 10):
+                    turn_table(1, (n - 6) // 2)
+                if batch_done and at == 3:
+                    multiply(done, 0)
+                if batch_done and at == 4:
+                    multiply(done, 1)
+                if batch_done and at == 5:
+                    multiply(done + 1, 0)
+                if 1 < p and last_of_batch(p - 2) and at == 0:
+                    multiply(done - 1, 1)
+                turn_q(n + 2)
+
+                products(n)
+                if n == 1:
+                    keep_cos(0, 1)
+                    keep_sin(0, 1)
+                if n == 3:
+                    keep_cos(0, 2)
+                    keep_sin(0, 2)
+                regroup(n - 1)
+                if n in (7, 9, 11):
+                    keep_cos(1, (n - 7) // 2)
+                    keep_sin(1, (n - 7) // 2)
+                if n == 3:
+                    group_q(1)
+                    rope_flat(1)
+                if n >= PER_PAIR and at in (0, 3):
+                    group_q(first + at // 3)
+                if n == 8:
+                    group_table(1, 0)
+                if n == 10:
+                    group_table(1, 1)
+                if p < len(PAIRS) and last_of_batch(p) and at == 4:
+                    group_v(PAIRS[p][0])
+                if p < len(PAIRS) and last_of_batch(p) and at == 5:
+                    quantise_v(PAIRS[p][0])
+                if 0 < p and at == 1:
+                    quantise(done)
+                if 0 < p and at == 4:
+                    quantise(done + 1)
+                if n >= PER_PAIR and at in (1, 4):
+                    rest_of_flat = rope_flat(first + at // 3)
+                if batch_done and at == 4:
+                    add_state(done, 0)
+                if batch_done and at == 5:
+                    add_state(done, 1)
+                if 1 < p and last_of_batch(p - 2) and at == 0:
+                    add_state(done - 1, 0)
+                if 1 < p and last_of_batch(p - 2) and at == 1:
+                    add_state(done - 1, 1)
+            last = ROUNDS - 1
+            quantise(last - 1)
+            sums(STEPS - 1)
+            multiply(last - 1, 0)
+            quantise(last, 0, 2)
+            regroup(STEPS - 1)
+            product, combine = rest_of_flat
+            product(0, 1, nc.vector)
+            product(1, 1, nc.vector)
+            add_state(last - 1, 0)
+            combine(1, nc.vector)
+            multiply(last - 1, 1)
+            add_state(last - 1, 1)
+            multiply(last, 0)
+            quantise(last, 1, 2)
+            add_state(last, 0)
+            multiply(last, 1)
+            add_state(last, 1)

@@ -21,7 +21,7 @@ PASSES = T // K_PASS
 W_UNIT = 2 * P
 UNITS = N // W_UNIT
 TURNED = UNITS - 1
-PAIRS = [(0, 0), (1, 0), (0, 1), (1, 1), (2, 1), (2, 0), (3, 0), (3, 1)]
+PAIRS = [(0, 0), (1, 0), (2, 0), (0, 1), (1, 1), (2, 1), (3, 1), (3, 0)]
 ROUNDS = NH * len(PAIRS)
 PER_PAIR = NH * TURNED
 STEPS = PER_PAIR * len(PAIRS)
@@ -50,15 +50,13 @@ def tile_attention_pb_t_kernel(tc, Q, V, state, cos, sin, out):
     nc = tc.nc
     with ExitStack() as ctx:
         keep = ctx.enter_context(tc.tile_pool(name="keep", bufs=1))
-        raw_pool = ctx.enter_context(tc.tile_pool(name="table_raw", bufs=6))
         turned_pool = ctx.enter_context(tc.tile_pool(name="turned", bufs=PASSES * TURNED))
         flat_pool = ctx.enter_context(tc.tile_pool(name="flat", bufs=PASSES))
-        q_pool = ctx.enter_context(tc.tile_pool(name="q_raw", bufs=5))
-        first_q_pool = ctx.enter_context(tc.tile_pool(name="first_q", bufs=6))
+        q_pool = ctx.enter_context(tc.tile_pool(name="q_raw", bufs=7))
         qg_pool = ctx.enter_context(tc.tile_pool(name="q_grouped", bufs=3))
         prod_pool = ctx.enter_context(tc.tile_pool(name="products", bufs=3))
         g_pool = ctx.enter_context(tc.tile_pool(name="grouped", bufs=5))
-        code_pool = ctx.enter_context(tc.tile_pool(name="codes", bufs=7))
+        code_pool = ctx.enter_context(tc.tile_pool(name="codes", bufs=10))
         v_pool = ctx.enter_context(tc.tile_pool(name="v", bufs=2))
         state_pool = ctx.enter_context(tc.tile_pool(name="state", bufs=4))
         res_pool = ctx.enter_context(tc.tile_pool(name="res", bufs=2))
@@ -69,39 +67,42 @@ def tile_attention_pb_t_kernel(tc, Q, V, state, cos, sin, out):
         ident = keep.tile([P, P], F32)
         make_identity(nc, ident[:])
 
-        q_of, qg_of, raw_of, bank_of, table_of, qt_of, prod_of = {}, {}, {}, {}, {}, {}, {}
+        first_of, q_of, qg_of, raw_of, bank_of, table_of, qt_of, prod_of = {}, {}, {}, {}, {}, {}, {}, {}
         flat_of, sum_of, grouped_of, codes_of, acc_of, v_of, state_of, res_of = {}, {}, {}, {}, {}, {}, {}, {}
 
-        def load_table(c, k0, k1):
-            tokens = slice(c * K_PASS, (c + 1) * K_PASS)
-            for k in range(k0, k1):
-                raw_of[(c, k)] = []
-            for table in (cos, sin):
-                table_raw = (raw_pool if c == 0 else q_pool).tile(
-                    [P, PACK, (k1 - k0) * W_UNIT], BF16, name="table_raw" if c == 0 else "q_raw"
-                )
-                for k in range(k0, k1):
-                    raw_of[(c, k)].append(table_raw[:, :, (k - k0) * W_UNIT : (k - k0 + 1) * W_UNIT])
-                nc.sync.dma_start(
-                    out=table_raw[:],
-                    in_=table[tokens, k0 * W_UNIT : k1 * W_UNIT].rearrange("(p j) w -> p j w", j=PACK),
-                )
+        def rows(table, c, k0, k1):
+            return table[c * K_PASS : (c + 1) * K_PASS, k0 * W_UNIT : k1 * W_UNIT].rearrange(
+                "(p j) w -> p j w", j=PACK
+            )
 
-        def load_q(r, k0, k1):
-            if r >= ROUNDS:
-                return
+        def load_first(k, sources):
+            if k not in first_of:
+                q_raw = q_pool.tile([P, NH + 2, PACK, W_UNIT], BF16)
+                first_of[k] = q_raw
+                raw_of[(0, k)] = [q_raw[:, 0], q_raw[:, 1]]
+                for h in range(NH):
+                    q_of[(h, k)] = q_raw[:, 2 + h]
+            b, c = PAIRS[0]
+            for s in sources:
+                table = (cos, sin, Q[b, 0], Q[b, 1])[s]
+                nc.sync.dma_start(out=first_of[k][:, s], in_=rows(table, c, k, k + 1))
+
+        def load_units(table):
+            q_raw = q_pool.tile([P, PACK, N], BF16)
+            nc.sync.dma_start(out=q_raw[:], in_=table)
+            return [q_raw[:, :, k * W_UNIT : (k + 1) * W_UNIT] for k in range(UNITS)]
+
+        def load_table(c):
+            cos_units = load_units(rows(cos, c, 0, UNITS))
+            sin_units = load_units(rows(sin, c, 0, UNITS))
+            for k in range(UNITS):
+                raw_of[(c, k)] = [cos_units[k], sin_units[k]]
+
+        def load_q(r):
             b, h, c = place(r)
-            q_raw = (first_q_pool if r < NH else q_pool).tile(
-                [P, PACK, (k1 - k0) * W_UNIT], BF16, name="q_raw"
-            )
-            for k in range(k0, k1):
-                q_of[(r, k)] = q_raw[:, :, (k - k0) * W_UNIT : (k - k0 + 1) * W_UNIT]
-            nc.sync.dma_start(
-                out=q_raw[:],
-                in_=Q[
-                    b, h, c * K_PASS : (c + 1) * K_PASS, k0 * W_UNIT : k1 * W_UNIT
-                ].rearrange("(p j) w -> p j w", j=PACK),
-            )
+            units = load_units(rows(Q[b, h], c, 0, UNITS))
+            for k in range(UNITS):
+                q_of[(r, k)] = units[k]
 
         def load_state(r):
             b, h, c = place(r)
@@ -113,14 +114,14 @@ def tile_attention_pb_t_kernel(tc, Q, V, state, cos, sin, out):
             )
 
         def load_v(b):
-            v_raw = v_pool.tile([P, PASSES, PACK, D], BF16)
+            v_raw = v_pool.tile([P, PASSES, PACK, D], BF16, bufs=1)
             nc.sync.dma_start(
                 out=v_raw[:], in_=V[b, 0].rearrange("(c p j) d -> p c j d", p=P, j=PACK)
             )
             v_of[b] = [v_raw]
 
         def group_v(b):
-            v_grouped = v_pool.tile([P, PASSES, D, PACK], BF16, align_bytes=64)
+            v_grouped = v_pool.tile([P, PASSES, D, PACK], BF16, align_bytes=64, bufs=1)
             nc.scalar.copy(out=v_grouped[:], in_=v_of[b][0][:].rearrange("p c j d -> p c d j"))
             v_of[b].append(v_grouped)
 
@@ -134,39 +135,42 @@ def tile_attention_pb_t_kernel(tc, Q, V, state, cos, sin, out):
             )
             v_of[b] = (v_codes, v_scales)
 
-        def turn_table(c, k):
-            bank_of[(c, k)] = []
-            for which in range(2):
-                bank = sum_psum.tile([P, PACK, P], F32, tag="sum")
-                for j in range(PACK):
-                    nc.tensor.transpose(
-                        bank[:, j, :], raw_of[(c, k)][which][:, j, :].bitcast(F32), ident[:]
-                    )
-                bank_of[(c, k)].append(
-                    bank[:].rearrange("i j p -> i (j p)").bitcast(BF16)
-                    .rearrange("i (x ab) -> i ab x", ab=2)
+        def turn_table(c, k, which):
+            bank = sum_psum.tile([P, PACK, P], F32, tag="sum")
+            for j in range(PACK):
+                nc.tensor.transpose(
+                    bank[:, j, :], raw_of[(c, k)][which][:, j, :].bitcast(F32), ident[:]
                 )
+            bank_of[(c, k, which)] = (
+                bank[:].rearrange("i j p -> i (j p)").bitcast(BF16)
+                .rearrange("i (x ab) -> i ab x", ab=2)
+            )
 
-        def keep_cos(c, k):
-            table_t = turned_pool.tile([P, 2, 2, K_PASS], BF16)
-            table_of[(c, k)] = table_t
-            if c == 0:
-                nc.vector.tensor_copy(out=table_t[:, 0], in_=bank_of[(c, k)][0])
-            else:
-                nc.scalar.copy(out=table_t[:, 0], in_=bank_of[(c, k)][0])
-
-        def keep_sin(c, k):
+        def keep_table(c, k, which):
+            by_parity = bank_of[(c, k, which)]
+            if (c, k) not in table_of:
+                table_t = turned_pool.tile([P, 2, 2, K_PASS], BF16)
+                table_of[(c, k)] = table_t
             table_t = table_of[(c, k)]
-            by_parity = bank_of[(c, k)][1]
-            nc.scalar.copy(out=table_t[:, 1, 0, :], in_=by_parity[:, 1])
-            nc.scalar.mul(out=table_t[:, 1, 1, :], in_=by_parity[:, 0], mul=-1.0)
+            if which == 1:
+                nc.scalar.copy(out=table_t[:, 1, 0, :], in_=by_parity[:, 1])
+                nc.scalar.mul(out=table_t[:, 1, 1, :], in_=by_parity[:, 0], mul=-1.0)
+            elif c == 0:
+                nc.vector.tensor_copy(out=table_t[:, 0], in_=by_parity)
+            else:
+                nc.scalar.copy(out=table_t[:, 0], in_=by_parity)
 
         def group_table(c, which):
             if (c, TURNED) not in table_of:
                 table_g = flat_pool.tile([P, 2, 2, P, PACK], BF16)
                 table_of[(c, TURNED)] = table_g
+            table_g = table_of[(c, TURNED)]
             by_parity = raw_of[(c, TURNED)][which].rearrange("p j (i ab) -> p ab i j", ab=2)
-            nc.scalar.copy(out=table_of[(c, TURNED)][:, which], in_=by_parity)
+            if which == 0:
+                nc.scalar.copy(out=table_g[:, 0], in_=by_parity)
+            else:
+                nc.scalar.copy(out=table_g[:, 1, 0], in_=by_parity[:, 1])
+                nc.scalar.mul(out=table_g[:, 1, 1], in_=by_parity[:, 0], mul=-1.0)
 
         def group_q(r):
             if r >= ROUNDS:
@@ -214,35 +218,36 @@ def tile_attention_pb_t_kernel(tc, Q, V, state, cos, sin, out):
             return grouped_of[r]
 
         def rope_flat(r):
-            if r >= ROUNDS:
-                return
-            table_g = table_of[(place(r)[2], TURNED)]
             grouped = grouped_tile(r)
             flat = flat_of[r]
+            table_g = table_of[(place(r)[2], TURNED)]
 
-            def product(which, ab, engine=nc.gpsimd):
+            def product(engine, which, ab):
                 engine.tensor_tensor(
-                    out=flat[:, which, ab],
-                    in0=qg_of[r][:, ab if which == 0 else 1 - ab],
-                    in1=table_g[:, which, ab],
+                    out=flat[:, which, ab], in0=qg_of[r][:, ab], in1=table_g[:, which, ab],
                     op=ALU.mult,
                 )
 
-            def combine(ab, engine=nc.gpsimd):
+            def combine(engine, ab):
                 engine.tensor_tensor(
-                    out=grouped[:, TURNED, ab], in0=flat[:, 0, ab], in1=flat[:, 1, ab],
-                    op=ALU.subtract if ab == 0 else ALU.add,
+                    out=grouped[:, TURNED, ab], in0=flat[:, 0, ab], in1=flat[:, 1, 1 - ab],
+                    op=ALU.add,
                 )
 
-            product(0, 0)
-            product(1, 0)
-            if r == ROUNDS - 1:
-                combine(0)
-                return product, combine
-            product(0, 1)
-            combine(0)
-            product(1, 1)
-            combine(1)
+            if r < ROUNDS - 1:
+                nc.gpsimd.tensor_tensor(
+                    out=flat[:],
+                    in0=qg_of[r][:].unsqueeze(1).broadcast_to([P, 2, 2, P, PACK]),
+                    in1=table_g[:],
+                    op=ALU.mult,
+                )
+                combine(nc.gpsimd, 0)
+                combine(nc.gpsimd, 1)
+            else:
+                product(nc.gpsimd, 0, 0)
+                product(nc.gpsimd, 1, 1)
+                combine(nc.gpsimd, 0)
+            return product, combine
 
         def sums(n):
             if n < 0 or n >= STEPS:
@@ -329,49 +334,46 @@ def tile_attention_pb_t_kernel(tc, Q, V, state, cos, sin, out):
             )
 
         with tc.manual_schedule():
-            load_table(0, 0, 1)
-            load_q(0, 0, 1)
-            load_q(1, 0, 1)
-            load_table(0, TURNED, UNITS)
-            load_q(0, TURNED, UNITS)
-            load_table(0, 1, 2)
-            load_q(0, 1, 2)
-            load_q(1, 1, 2)
-            load_table(0, 2, 3)
-            load_q(0, 2, 3)
-            load_q(1, 2, 3)
-            load_q(1, TURNED, UNITS)
-            load_q(2, 0, UNITS)
-            load_q(3, 0, UNITS)
-            load_table(1, 0, UNITS)
-            turn_table(0, 0)
-            keep_cos(0, 0)
-            keep_sin(0, 0)
+            load_first(0, (0, 1, 2, 3))
+            load_first(TURNED, (0, 1, 2))
+            load_first(1, (0, 1, 2, 3))
+            load_first(2, (0, 1, 2, 3))
+            load_first(TURNED, (3,))
+            load_q(2)
+            load_q(3)
+            load_table(1)
+            load_q(4)
+            load_q(5)
+            for which in range(2):
+                turn_table(0, 0, which)
+                keep_table(0, 0, which)
             turn_q(0)
             turn_q(1)
-            turn_table(0, 1)
+            for which in range(2):
+                turn_table(0, 1, which)
             group_table(0, 0)
             group_table(0, 1)
             group_q(0)
             rope_flat(0)
+            second_table = [(k, which) for k in range(TURNED) for which in range(2)]
             for n in range(STEPS):
                 p, at = divmod(n, PER_PAIR)
                 first = NH * p
                 done = first - NH
                 batch_done = 0 < p and last_of_batch(p - 1)
-                if at == 0 and 1 < p + 1 < len(PAIRS):
-                    load_q(first + 2, 0, UNITS)
-                    load_q(first + 3, 0, UNITS)
-                if at == 1 and p < len(PAIRS) and last_of_batch(p):
+                if at in (0, 3) and 3 <= p + 2 < len(PAIRS):
+                    load_q(first + 4 + at // 3)
+                if at == 1 and last_of_batch(p):
                     load_state(first)
                     load_state(first + 1)
                     load_v(PAIRS[p][0])
 
                 sums(n - 1)
                 if n == 2:
-                    turn_table(0, 2)
-                if n in (6, 8, 10):
-                    turn_table(1, (n - 6) // 2)
+                    turn_table(0, 2, 0)
+                    turn_table(0, 2, 1)
+                if PER_PAIR <= n and n % 3 > 0 and second_table:
+                    turn_table(1, *second_table[0])
                 if batch_done and at == 3:
                     multiply(done, 0)
                 if batch_done and at == 4:
@@ -384,34 +386,31 @@ def tile_attention_pb_t_kernel(tc, Q, V, state, cos, sin, out):
 
                 products(n)
                 if n == 1:
-                    keep_cos(0, 1)
-                    keep_sin(0, 1)
+                    keep_table(0, 1, 0)
+                    keep_table(0, 1, 1)
                 if n == 3:
-                    keep_cos(0, 2)
-                    keep_sin(0, 2)
+                    keep_table(0, 2, 0)
+                    keep_table(0, 2, 1)
                 regroup(n - 1)
-                if n in (7, 9, 11):
-                    keep_cos(1, (n - 7) // 2)
-                    keep_sin(1, (n - 7) // 2)
+                if PER_PAIR <= n and n % 3 > 0 and second_table:
+                    keep_table(1, *second_table.pop(0))
                 if n == 3:
                     group_q(1)
                     rope_flat(1)
                 if n >= PER_PAIR and at in (0, 3):
                     group_q(first + at // 3)
-                if n == 8:
-                    group_table(1, 0)
-                if n == 10:
-                    group_table(1, 1)
-                if p < len(PAIRS) and last_of_batch(p) and at == 4:
+                if n in (16, 17):
+                    group_table(1, n - 16)
+                if last_of_batch(p) and at == 2:
                     group_v(PAIRS[p][0])
-                if p < len(PAIRS) and last_of_batch(p) and at == 5:
-                    quantise_v(PAIRS[p][0])
                 if 0 < p and at == 1:
                     quantise(done)
                 if 0 < p and at == 4:
                     quantise(done + 1)
+                    if last_of_batch(p):
+                        quantise_v(PAIRS[p][0])
                 if n >= PER_PAIR and at in (1, 4):
-                    rest_of_flat = rope_flat(first + at // 3)
+                    product, combine = rope_flat(first + at // 3)
                 if batch_done and at == 4:
                     add_state(done, 0)
                 if batch_done and at == 5:
@@ -426,11 +425,10 @@ def tile_attention_pb_t_kernel(tc, Q, V, state, cos, sin, out):
             multiply(last - 1, 0)
             quantise(last, 0, 2)
             regroup(STEPS - 1)
-            product, combine = rest_of_flat
-            product(0, 1, nc.vector)
-            product(1, 1, nc.vector)
+            product(nc.vector, 0, 1)
+            product(nc.vector, 1, 0)
             add_state(last - 1, 0)
-            combine(1, nc.vector)
+            combine(nc.vector, 1)
             multiply(last - 1, 1)
             add_state(last - 1, 1)
             multiply(last, 0)

@@ -234,19 +234,14 @@ def tile_attention_pb_t_kernel(tc, Q, V, state, cos, sin, out):
                     op=ALU.add,
                 )
 
+            product(nc.gpsimd, 0, 0)
+            product(nc.gpsimd, 1, 1)
             if r < ROUNDS - 1:
-                nc.gpsimd.tensor_tensor(
-                    out=flat[:],
-                    in0=qg_of[r][:].unsqueeze(1).broadcast_to([P, 2, 2, P, PACK]),
-                    in1=table_g[:],
-                    op=ALU.mult,
-                )
-                combine(nc.gpsimd, 0)
+                product(nc.gpsimd, 0, 1)
+            combine(nc.gpsimd, 0)
+            if r < ROUNDS - 1:
+                product(nc.gpsimd, 1, 0)
                 combine(nc.gpsimd, 1)
-            else:
-                product(nc.gpsimd, 0, 0)
-                product(nc.gpsimd, 1, 1)
-                combine(nc.gpsimd, 0)
             return product, combine
 
         def sums(n):
@@ -364,9 +359,10 @@ def tile_attention_pb_t_kernel(tc, Q, V, state, cos, sin, out):
                 if at in (0, 3) and 3 <= p + 2 < len(PAIRS):
                     load_q(first + 4 + at // 3)
                 if at == 1 and last_of_batch(p):
+                    load_v(PAIRS[p][0])
+                if at == 5 and last_of_batch(p):
                     load_state(first)
                     load_state(first + 1)
-                    load_v(PAIRS[p][0])
 
                 sums(n - 1)
                 if n == 2:

@@ -234,14 +234,17 @@ def tile_attention_pb_t_kernel(tc, Q, V, state, cos, sin, out):
                     op=ALU.add,
                 )
 
-            product(nc.gpsimd, 0, 0)
-            product(nc.gpsimd, 1, 1)
             if r < ROUNDS - 1:
-                product(nc.gpsimd, 0, 1)
-            combine(nc.gpsimd, 0)
-            if r < ROUNDS - 1:
-                product(nc.gpsimd, 1, 0)
+                for which in range(2):
+                    nc.gpsimd.tensor_tensor(
+                        out=flat[:, which], in0=qg_of[r][:], in1=table_g[:, which], op=ALU.mult
+                    )
+                combine(nc.gpsimd, 0)
                 combine(nc.gpsimd, 1)
+            else:
+                product(nc.gpsimd, 0, 0)
+                product(nc.gpsimd, 1, 1)
+                combine(nc.gpsimd, 0)
             return product, combine
 
         def sums(n):

@@ -56,7 +56,7 @@ def tile_attention_pb_t_kernel(tc, Q, V, state, cos, sin, out):
         qg_pool = ctx.enter_context(tc.tile_pool(name="q_grouped", bufs=3))
         prod_pool = ctx.enter_context(tc.tile_pool(name="products", bufs=3))
         g_pool = ctx.enter_context(tc.tile_pool(name="grouped", bufs=5))
-        code_pool = ctx.enter_context(tc.tile_pool(name="codes", bufs=10))
+        code_pool = ctx.enter_context(tc.tile_pool(name="codes", bufs=9))
         v_pool = ctx.enter_context(tc.tile_pool(name="v", bufs=2))
         state_pool = ctx.enter_context(tc.tile_pool(name="state", bufs=4))
         res_pool = ctx.enter_context(tc.tile_pool(name="res", bufs=2))
@@ -335,8 +335,8 @@ def tile_attention_pb_t_kernel(tc, Q, V, state, cos, sin, out):
             load_first(0, (0, 1, 2, 3))
             load_first(TURNED, (0, 1, 2))
             load_first(1, (0, 1, 2, 3))
-            load_first(2, (0, 1, 2, 3))
             load_first(TURNED, (3,))
+            load_first(2, (0, 1, 2, 3))
             load_q(2)
             load_q(3)
             load_table(1)
@@ -393,22 +393,24 @@ def tile_attention_pb_t_kernel(tc, Q, V, state, cos, sin, out):
                 regroup(n - 1)
                 if PER_PAIR <= n and n % 3 > 0 and second_table:
                     keep_table(1, *second_table.pop(0))
-                if n == 3:
+                if n == 2:
                     group_q(1)
                     rope_flat(1)
-                if n >= PER_PAIR and at in (0, 3):
+                if n in (5, 8):
+                    group_q(2 + n // 8)
+                if p > 1 and at in (0, 3):
                     group_q(first + at // 3)
                 if n in (16, 17):
                     group_table(1, n - 16)
                 if last_of_batch(p) and at == 2:
                     group_v(PAIRS[p][0])
-                if 0 < p and at == 1:
+                if n == PER_PAIR or p > 1 and at == 1:
                     quantise(done)
-                if 0 < p and at == 4:
+                if n == PER_PAIR + 3 or p > 1 and at == 4:
                     quantise(done + 1)
                     if last_of_batch(p):
                         quantise_v(PAIRS[p][0])
-                if n >= PER_PAIR and at in (1, 4):
+                if p == 1 and at in (0, 3) or p > 1 and at in (1, 4):
                     product, combine = rope_flat(first + at // 3)
                 if batch_done and at == 4:
                     add_state(done, 0)

@@ -182,6 +182,18 @@ def tile_attention_pb_t_kernel(tc, Q, V, state, cos, sin, out):
                 in_=q_of[(r, TURNED)].rearrange("p j (i ab) -> p ab i j", ab=2),
             )
 
+        def keep_clock(r, bank):
+            codes, scales = codes_of[r]
+            nc.tensor.matmul_mx(
+                out=bank[:].rearrange("p j i -> p (j i)"),
+                lhsT=codes[:, TURNED, 0, :].bitcast(FP8X4),
+                lhsT_scale=scales[:, TURNED, 0, :],
+                rhs=codes[:, 0:2].rearrange("p k ab i -> p (k ab i)").bitcast(FP8X4),
+                rhs_scale=scales[:, 0:2].rearrange("p k ab i -> p (k ab i)"),
+                start=True,
+                stop=True,
+            )
+
         def turn_q(n):
             if n >= STEPS:
                 return
@@ -251,10 +263,11 @@ def tile_attention_pb_t_kernel(tc, Q, V, state, cos, sin, out):
             if n < 0 or n >= STEPS:
                 return
             prod = prod_of[n]
-            sum_of[n] = []
             for ab in range(2):
-                acc_sum = sum_psum.tile([P, PACK, P], F32, tag="sum")
-                sum_of[n].append(acc_sum)
+                if ab == len(sum_of.setdefault(n, [])):
+                    acc_sum = sum_psum.tile([P, PACK, P], F32, tag="sum")
+                    sum_of[n].append(acc_sum)
+                acc_sum = sum_of[n][ab]
                 for j in range(PACK):
                     tokens = slice(j * P, (j + 1) * P)
                     nc.tensor.matmul(
@@ -381,6 +394,10 @@ def tile_attention_pb_t_kernel(tc, Q, V, state, cos, sin, out):
                     multiply(done + 1, 0)
                 if 1 < p and last_of_batch(p - 2) and at == 0:
                     multiply(done - 1, 1)
+                if (batch_done and at in (3, 4, 5) or 1 < p and last_of_batch(p - 2) and at == 0):
+                    acc_sum = sum_psum.tile([P, PACK, P], F32, tag="sum")
+                    sum_of[n] = [acc_sum]
+                    keep_clock(done - NH if at == 0 else done, acc_sum)
                 turn_q(n + 2)
 
                 products(n)

@@ -46,6 +46,10 @@ def last_of_batch(p):
     return PAIRS[p][0] in [b for b, c in PAIRS[:p]]
 
 
+def helped(r):
+    return 2 * NH <= r <= 4 * NH
+
+
 def tile_attention_pb_t_kernel(tc, Q, V, state, cos, sin, out):
     nc = tc.nc
     with ExitStack() as ctx:
@@ -252,7 +256,8 @@ def tile_attention_pb_t_kernel(tc, Q, V, state, cos, sin, out):
                         out=flat[:, which], in0=qg_of[r][:], in1=table_g[:, which], op=ALU.mult
                     )
                 combine(nc.gpsimd, 0)
-                combine(nc.gpsimd, 1)
+                if not helped(r):
+                    combine(nc.gpsimd, 1)
             else:
                 product(nc.gpsimd, 0, 0)
                 product(nc.gpsimd, 1, 1)
@@ -422,8 +427,12 @@ def tile_attention_pb_t_kernel(tc, Q, V, state, cos, sin, out):
                 if last_of_batch(p) and at == 2:
                     group_v(PAIRS[p][0])
                 if n == PER_PAIR or p > 1 and at == 1:
+                    if helped(done + 1):
+                        combine(nc.vector, 1)
                     quantise(done)
                 if n == PER_PAIR + 3 or p > 1 and at == 4:
+                    if helped(first):
+                        combine(nc.vector, 1)
                     quantise(done + 1)
                     if last_of_batch(p):
                         quantise_v(PAIRS[p][0])

from contextlib import ExitStack

import concourse.mybir as mybir
from concourse.masks import make_identity

F32 = mybir.dt.float32
BF16 = mybir.dt.bfloat16
U32 = mybir.dt.uint32
U8 = mybir.dt.uint8
FP8X4 = mybir.dt.float8_e4m3fn_x4
ALU = mybir.AluOpType

B, NH, T, D, N = 4, 2, 1024, 128, 1024
SCALE = N**-0.5
FLOPS = 2 * B * NH * T * N * D

P = 128
PACK = 4
K_PASS = P * PACK
PASSES = T // K_PASS
W_UNIT = 2 * P
UNITS = N // W_UNIT
TURNED = UNITS - 1
PAIRS = [(0, 0), (1, 0), (2, 0), (0, 1), (1, 1), (2, 1), (3, 1), (3, 0)]
ROUNDS = NH * len(PAIRS)
PER_PAIR = NH * TURNED
STEPS = PER_PAIR * len(PAIRS)


def place(r):
    p, h = divmod(r, NH)
    b, c = PAIRS[p]
    return b, h, c


def step(n):
    p, rest = divmod(n, PER_PAIR)
    if p == len(PAIRS) - 1:
        h, k = divmod(rest, TURNED)
    else:
        k, h = divmod(rest, NH)
    return p * NH + h, k


def last_of_batch(p):
    return PAIRS[p][0] in [b for b, c in PAIRS[:p]]


def helped(r):
    return 2 * NH <= r <= 4 * NH


def tile_attention_pb_t_kernel(tc, Q, V, state, cos, sin, out):
    nc = tc.nc
    with ExitStack() as ctx:
        keep = ctx.enter_context(tc.tile_pool(name="keep", bufs=1))
        turned_pool = ctx.enter_context(tc.tile_pool(name="turned", bufs=PASSES * TURNED))
        flat_pool = ctx.enter_context(tc.tile_pool(name="flat", bufs=PASSES))
        q_pool = ctx.enter_context(tc.tile_pool(name="q_raw", bufs=7))
        qg_pool = ctx.enter_context(tc.tile_pool(name="q_grouped", bufs=3))
        prod_pool = ctx.enter_context(tc.tile_pool(name="products", bufs=3))
        g_pool = ctx.enter_context(tc.tile_pool(name="grouped", bufs=5))
        code_pool = ctx.enter_context(tc.tile_pool(name="codes", bufs=9))
        v_pool = ctx.enter_context(tc.tile_pool(name="v", bufs=2))
        state_pool = ctx.enter_context(tc.tile_pool(name="state", bufs=4))
        res_pool = ctx.enter_context(tc.tile_pool(name="res", bufs=2))
        qt_psum = ctx.enter_context(tc.psum_pool(name="qt_psum", bufs=2))
        sum_psum = ctx.enter_context(tc.psum_pool(name="sum_psum", bufs=4))
        acc_psum = ctx.enter_context(tc.psum_pool(name="acc_psum", bufs=2))

        ident = keep.tile([P, P], F32)
        make_identity(nc, ident[:])

        first_of, q_of, qg_of, raw_of, bank_of, table_of, qt_of, prod_of = {}, {}, {}, {}, {}, {}, {}, {}
        flat_of, sum_of, grouped_of, codes_of, acc_of, v_of, state_of, res_of = {}, {}, {}, {}, {}, {}, {}, {}

        def rows(table, c, k0, k1):
            return table[c * K_PASS : (c + 1) * K_PASS, k0 * W_UNIT : k1 * W_UNIT].rearrange(
                "(p j) w -> p j w", j=PACK
            )

        def load_first(k, sources):
            if k not in first_of:
                q_raw = q_pool.tile([P, NH + 2, PACK, W_UNIT], BF16)
                first_of[k] = q_raw
                raw_of[(0, k)] = [q_raw[:, 0], q_raw[:, 1]]
                for h in range(NH):
                    q_of[(h, k)] = q_raw[:, 2 + h]
            b, c = PAIRS[0]
            for s in sources:
                table = (cos, sin, Q[b, 0], Q[b, 1])[s]
                nc.sync.dma_start(out=first_of[k][:, s], in_=rows(table, c, k, k + 1))

        def load_units(table):
            q_raw = q_pool.tile([P, PACK, N], BF16)
            nc.sync.dma_start(out=q_raw[:], in_=table)
            return [q_raw[:, :, k * W_UNIT : (k + 1) * W_UNIT] for k in range(UNITS)]

        def load_table(c):
            cos_units = load_units(rows(cos, c, 0, UNITS))
            sin_units = load_units(rows(sin, c, 0, UNITS))
            for k in range(UNITS):
                raw_of[(c, k)] = [cos_units[k], sin_units[k]]

        def load_q(r):
            b, h, c = place(r)
            units = load_units(rows(Q[b, h], c, 0, UNITS))
            for k in range(UNITS):
                q_of[(r, k)] = units[k]

        def load_state(r):
            b, h, c = place(r)
            state_sb = state_pool.tile([P, UNITS, 2, D], BF16)
            state_of[r] = state_sb
            nc.sync.dma_start(
                out=state_sb[:],
                in_=state[b, h].rearrange("(k i ab) d -> i k ab d", k=UNITS, ab=2),
            )

        def load_v(b):
            v_raw = v_pool.tile([P, PASSES, PACK, D], BF16, bufs=1)
            nc.sync.dma_start(
                out=v_raw[:], in_=V[b, 0].rearrange("(c p j) d -> p c j d", p=P, j=PACK)
            )
            v_of[b] = [v_raw]

        def group_v(b):
            v_grouped = v_pool.tile([P, PASSES, D, PACK], BF16, align_bytes=64, bufs=1)
            nc.scalar.copy(out=v_grouped[:], in_=v_of[b][0][:].rearrange("p c j d -> p c d j"))
            v_of[b].append(v_grouped)

        def quantise_v(b):
            v_codes = v_pool.tile([P, PASSES, D], U32, align_bytes=64)
            v_scales = v_pool.tile([P, PASSES, D], U8, align_bytes=64)
            nc.vector.quantize_mx(
                out=v_codes[:].rearrange("p c d -> p (c d)").bitcast(FP8X4),
                scales=v_scales[:].rearrange("p c d -> p (c d)"),
                in_=v_of[b][1][:].rearrange("p c d j -> p (c d j)"),
            )
            v_of[b] = (v_codes, v_scales)

        def turn_table(c, k, which):
            bank = sum_psum.tile([P, PACK, P], F32, tag="sum")
            for j in range(PACK):
                nc.tensor.transpose(
                    bank[:, j, :], raw_of[(c, k)][which][:, j, :].bitcast(F32), ident[:]
                )
            bank_of[(c, k, which)] = (
                bank[:].rearrange("i j p -> i (j p)").bitcast(BF16)
                .rearrange("i (x ab) -> i ab x", ab=2)
            )

        def keep_table(c, k, which):
            by_parity = bank_of[(c, k, which)]
            if (c, k) not in table_of:
                table_t = turned_pool.tile([P, 2, 2, K_PASS], BF16)
                table_of[(c, k)] = table_t
            table_t = table_of[(c, k)]
            if which == 1:
                nc.scalar.copy(out=table_t[:, 1, 0, :], in_=by_parity[:, 1])
                nc.scalar.mul(out=table_t[:, 1, 1, :], in_=by_parity[:, 0], mul=-1.0)
            elif c == 0:
                nc.vector.tensor_copy(out=table_t[:, 0], in_=by_parity)
            else:
                nc.scalar.copy(out=table_t[:, 0], in_=by_parity)

        def group_table(c, which):
            if (c, TURNED) not in table_of:
                table_g = flat_pool.tile([P, 2, 2, P, PACK], BF16)
                table_of[(c, TURNED)] = table_g
            table_g = table_of[(c, TURNED)]
            by_parity = raw_of[(c, TURNED)][which].rearrange("p j (i ab) -> p ab i j", ab=2)
            if which == 0:
                nc.scalar.copy(out=table_g[:, 0], in_=by_parity)
            else:
                nc.scalar.copy(out=table_g[:, 1, 0], in_=by_parity[:, 1])
                nc.scalar.mul(out=table_g[:, 1, 1], in_=by_parity[:, 0], mul=-1.0)

        def group_q(r):
            if r >= ROUNDS:
                return
            q_grouped = qg_pool.tile([P, 2, P, PACK], BF16)
            qg_of[r] = q_grouped
            nc.scalar.copy(
                out=q_grouped[:],
                in_=q_of[(r, TURNED)].rearrange("p j (i ab) -> p ab i j", ab=2),
            )

        def keep_clock(r, bank):
            codes, scales = codes_of[r]
            nc.tensor.matmul_mx(
                out=bank[:].rearrange("p j i -> p (j i)"),
                lhsT=codes[:, TURNED, 0, :].bitcast(FP8X4),
                lhsT_scale=scales[:, TURNED, 0, :],
                rhs=codes[:, 0:2].rearrange("p k ab i -> p (k ab i)").bitcast(FP8X4),
                rhs_scale=scales[:, 0:2].rearrange("p k ab i -> p (k ab i)"),
                start=True,
                stop=True,
            )

        def turn_q(n):
            if n >= STEPS:
                return
            r, k = step(n)
            qt = qt_psum.tile([P, K_PASS], F32)
            qt_of[n] = qt
            for j in range(PACK):
                nc.tensor.transpose(
                    qt[:, j * P : (j + 1) * P],
                    q_of[(r, k)][:, j, :].bitcast(F32),
                    ident[:],
                )

        def products(n):
            if n >= STEPS:
                return
            r, k = step(n)
            prod = prod_pool.tile([P, 2, 2, K_PASS], F32)
            prod_of[n] = prod
            q_rows = qt_of[n][:].bitcast(BF16).rearrange("i (x ab) -> i ab x", ab=2)
            nc.vector.tensor_tensor(
                out=prod[:],
                in0=q_rows.unsqueeze(1).broadcast_to([P, 2, 2, K_PASS]),
                in1=table_of[(place(r)[2], k)][:],
                op=ALU.mult,
            )

        def grouped_tile(r):
            if r not in grouped_of:
                grouped = g_pool.tile([P, UNITS, 2, P, PACK], BF16, align_bytes=64, tag="g")
                grouped_of[r] = grouped
                flat = g_pool.tile([P, 2, 2, P, PACK], F32, align_bytes=64, tag="g")
                flat_of[r] = flat
            return grouped_of[r]

        def rope_flat(r):
            grouped = grouped_tile(r)
            flat = flat_of[r]
            table_g = table_of[(place(r)[2], TURNED)]

            def product(engine, which, ab):
                engine.tensor_tensor(
                    out=flat[:, which, ab], in0=qg_of[r][:, ab], in1=table_g[:, which, ab],
                    op=ALU.mult,
                )

            def combine(engine, ab):
                engine.tensor_tensor(
                    out=grouped[:, TURNED, ab], in0=flat[:, 0, ab], in1=flat[:, 1, 1 - ab],
                    op=ALU.add,
                )

            if r < ROUNDS - 1:
                for which in range(2):
                    nc.gpsimd.tensor_tensor(
                        out=flat[:, which], in0=qg_of[r][:], in1=table_g[:, which], op=ALU.mult
                    )
                combine(nc.gpsimd, 0)
                if not helped(r):
                    combine(nc.gpsimd, 1)
            else:
                product(nc.gpsimd, 0, 0)
                product(nc.gpsimd, 1, 1)
                combine(nc.gpsimd, 0)
            return product, combine

        def sums(n):
            if n < 0 or n >= STEPS:
                return
            prod = prod_of[n]
            for ab in range(2):
                if ab == len(sum_of.setdefault(n, [])):
                    acc_sum = sum_psum.tile([P, PACK, P], F32, tag="sum")
                    sum_of[n].append(acc_sum)
                acc_sum = sum_of[n][ab]
                for j in range(PACK):
                    tokens = slice(j * P, (j + 1) * P)
                    nc.tensor.matmul(
                        acc_sum[:, j, :], prod[:, 0, ab, tokens], ident[:],
                        start=True, stop=False, is_transpose=True,
                    )
                    nc.tensor.matmul(
                        acc_sum[:, j, :], prod[:, 1, 1 - ab, tokens], ident[:],
                        start=False, stop=True, is_transpose=True,
                    )

        def regroup(n):
            if n < 0 or n >= STEPS:
                return
            r, k = step(n)
            grouped = grouped_tile(r)
            for ab in range(2):
                nc.scalar.copy(
                    out=grouped[:, k, ab], in_=sum_of[n][ab][:].rearrange("p j i -> p i j")
                )

        def quantise(r, part=0, parts=1):
            if part == 0:
                codes = code_pool.tile([P, UNITS, 2, P], U32, align_bytes=64)
                scales = code_pool.tile([P, UNITS, 2, P], U8, align_bytes=64)
                codes_of[r] = (codes, scales)
            codes, scales = codes_of[r]
            units = slice(part * UNITS // parts, (part + 1) * UNITS // parts)
            nc.vector.quantize_mx(
                out=codes[:, units].rearrange("p k ab i -> p (k ab i)").bitcast(FP8X4),
                scales=scales[:, units].rearrange("p k ab i -> p (k ab i)"),
                in_=grouped_of[r][:, units].rearrange("p k ab i j -> p (k ab i j)"),
            )

        def multiply(r, half):
            b, h, c = place(r)
            v_codes, v_scales = v_of[b]
            acc = acc_psum.tile([P, UNITS // 2, 2, D], F32)
            acc_of[(r, half)] = acc
            rounds = [s for s in range(r + 1) if place(s)[:2] == (b, h)]
            for k in range(UNITS // 2):
                unit = half * (UNITS // 2) + k
                for ab in range(2):
                    for s in rounds:
                        codes, scales = codes_of[s]
                        t = place(s)[2]
                        nc.tensor.matmul_mx(
                            out=acc[:, k, ab, :],
                            lhsT=codes[:, unit, ab, :].bitcast(FP8X4),
                            lhsT_scale=scales[:, unit, ab, :],
                            rhs=v_codes[:, t, :].bitcast(FP8X4),
                            rhs_scale=v_scales[:, t, :],
                            start=(s == rounds[0]),
                            stop=(s == rounds[-1]),
                        )

        def add_state(r, half):
            b, h, c = place(r)
            if half == 0:
                res = res_pool.tile([P, UNITS, 2, D], F32)
                res_of[r] = res
            res = res_of[r]
            units = slice(half * (UNITS // 2), (half + 1) * (UNITS // 2))
            nc.vector.scalar_tensor_tensor(
                out=res[:, units],
                in0=acc_of[(r, half)][:],
                scalar=SCALE,
                in1=state_of[r][:, units],
                op0=ALU.mult,
                op1=ALU.add,
            )
            nc.sync.dma_start(
                out=out[b, h].rearrange("(k i ab) d -> i k ab d", k=UNITS, ab=2)[:, units],
                in_=res[:, units],
            )

        with tc.manual_schedule():
            load_first(0, (0, 1, 2, 3))
            load_first(TURNED, (0, 1, 2))
            load_first(1, (0, 1, 2, 3))
            load_first(TURNED, (3,))
            load_first(2, (0, 1, 2, 3))
            load_q(2)
            load_q(3)
            load_table(1)
            load_q(4)
            load_q(5)
            for which in range(2):
                turn_table(0, 0, which)
                keep_table(0, 0, which)
            turn_q(0)
            turn_q(1)
            for which in range(2):
                turn_table(0, 1, which)
            group_table(0, 0)
            group_table(0, 1)
            group_q(0)
            rope_flat(0)
            second_table = [(k, which) for k in range(TURNED) for which in range(2)]
            for n in range(STEPS):
                p, at = divmod(n, PER_PAIR)
                first = NH * p
                done = first - NH
                batch_done = 0 < p and last_of_batch(p - 1)
                if at in (0, 3) and 3 <= p + 2 < len(PAIRS):
                    load_q(first + 4 + at // 3)
                if at == 1 and last_of_batch(p):
                    load_v(PAIRS[p][0])
                if at == 5 and last_of_batch(p):
                    load_state(first)
                    load_state(first + 1)

                sums(n - 1)
                if n == 2:
                    turn_table(0, 2, 0)
                    turn_table(0, 2, 1)
                if PER_PAIR <= n and n % 3 > 0 and second_table:
                    turn_table(1, *second_table[0])
                if batch_done and at == 3:
                    multiply(done, 0)
                if batch_done and at == 4:
                    multiply(done, 1)
                if batch_done and at == 5:
                    multiply(done + 1, 0)
                if 1 < p and last_of_batch(p - 2) and at == 0:
                    multiply(done - 1, 1)
                if (batch_done and at in (3, 4, 5) or 1 < p and last_of_batch(p - 2) and at == 0):
                    acc_sum = sum_psum.tile([P, PACK, P], F32, tag="sum")
                    sum_of[n] = [acc_sum]
                    keep_clock(done - NH if at == 0 else done, acc_sum)
                turn_q(n + 2)

                products(n)
                if n == 1:
                    keep_table(0, 1, 0)
                    keep_table(0, 1, 1)
                if n == 3:
                    keep_table(0, 2, 0)
                    keep_table(0, 2, 1)
                regroup(n - 1)
                if PER_PAIR <= n and n % 3 > 0 and second_table:
                    keep_table(1, *second_table.pop(0))
                if n == 2:
                    group_q(1)
                    rope_flat(1)
                if n in (5, 8):
                    group_q(2 + n // 8)
                if p > 1 and at in (0, 3):
                    group_q(first + at // 3)
                if n in (16, 17):
                    group_table(1, n - 16)
                if last_of_batch(p) and at == 2:
                    group_v(PAIRS[p][0])
                if n == PER_PAIR or p > 1 and at == 1:
                    if helped(done + 1):
                        combine(nc.vector, 1)
                    quantise(done)
                if n == PER_PAIR + 3 or p > 1 and at == 4:
                    if helped(first):
                        combine(nc.vector, 1)
                    quantise(done + 1)
                    if last_of_batch(p):
                        quantise_v(PAIRS[p][0])
                if p == 1 and at in (0, 3) or p > 1 and at in (1, 4):
                    product, combine = rope_flat(first + at // 3)
                if batch_done and at == 4:
                    add_state(done, 0)
                if batch_done and at == 5:
                    add_state(done, 1)
                if 1 < p and last_of_batch(p - 2) and at == 0:
                    add_state(done - 1, 0)
                if 1 < p and last_of_batch(p - 2) and at == 1:
                    add_state(done - 1, 1)
            last = ROUNDS - 1
            quantise(last - 1)
            sums(STEPS - 1)
            multiply(last - 1, 0)
            quantise(last, 0, 2)
            regroup(STEPS - 1)
            product(nc.vector, 0, 1)
            product(nc.vector, 1, 0)
            add_state(last - 1, 0)
            combine(nc.vector, 1)
            multiply(last - 1, 1)
            add_state(last - 1, 1)
            multiply(last, 0)
            quantise(last, 1, 2)
            add_state(last, 0)
            multiply(last, 1)
            add_state(last, 1)
